import numpy as np
import ml_dtypes


def mxq(x, axis, fmt="e4m3"):
    dtype, down = {"e4m3": (ml_dtypes.float8_e4m3fn, 7), "e5m2": (ml_dtypes.float8_e5m2, 14)}[fmt]
    v = np.moveaxis(np.asarray(x, np.float32).astype(ml_dtypes.bfloat16).astype(np.float64), axis, -1)
    blocks = v.reshape(v.shape[:-1] + (-1, 32))
    amax = np.abs(blocks).max(-1, keepdims=True)
    byte = np.maximum(np.where(amax > 0, np.frexp(amax)[1] - 1 + 127, 0) - down, 1)
    scale = np.exp2(byte - 127.0)
    codes = (blocks / scale).astype(np.float32).astype(dtype).astype(np.float64)
    return np.moveaxis((codes * scale).reshape(v.shape), -1, axis)


WIDE = False


def mx_kscale(k):
    if not WIDE:
        return np.ones(k)
    levels = np.array([10, -10, 5, -5, 0])
    a = np.random.permutation(np.resize(levels, k // 512 * 4)).reshape(k // 512, 4)
    idx = np.arange(k)
    return np.exp2(a[idx // 512, idx % 128 // 32])


BF16 = ml_dtypes.bfloat16


def bf(x):
    return np.asarray(x, np.float32).astype(BF16)


def f64(x):
    return np.asarray(x).astype(np.float64)


E2M1 = np.array([0.0, 0.5, 1.0, 1.5, 2.0, 3.0, 4.0, 6.0, -0.0, -0.5, -1.0, -1.5, -2.0, -3.0, -4.0, -6.0])


def pack_weight(w, fmt):
    k, n = w.shape
    w = f64(bf(w)).reshape(k // 32, 32, n)
    amax = np.abs(w).max(1)
    if fmt == "e4m3":
        byte = np.frexp(amax)[1] - 1 + 127 - 7
    else:
        mant, ex = np.frexp(amax / 6.0)
        byte = np.where(mant > 0.5, ex, ex - 1) + 127
    byte = np.clip(np.where(amax > 0, byte, 1), 1, 254)
    scaled = (w * np.exp2(127.0 - byte)[:, None, :]).reshape(k, n).astype(np.float32)
    by_word = np.ascontiguousarray(scaled.reshape(k // 512, 128, 4, n).transpose(0, 1, 3, 2))
    if fmt == "e4m3":
        words = by_word.astype(ml_dtypes.float8_e4m3fn).view(np.uint8)
    else:
        c = by_word.astype(ml_dtypes.float4_e2m1fn).view(np.uint8) & 0xF
        words = c[..., 0::2] | (c[..., 1::2] << 4)
    return np.ascontiguousarray(words), np.ascontiguousarray(byte.astype(np.uint8).reshape(k // 512, 16, n))


def unpack_weight(words, scales, fmt):
    g, p, n, _ = words.shape
    if fmt == "e4m3":
        vals = np.ascontiguousarray(words).view(ml_dtypes.float8_e4m3fn).astype(np.float64)
    else:
        nib = np.empty((g, p, n, 4), np.uint8)
        nib[..., 0::2] = words & 0xF
        nib[..., 1::2] = words >> 4
        vals = E2M1[nib]
    vals = vals * np.repeat(np.exp2(scales.astype(np.float64) - 127.0), 8, axis=1)[..., None]
    return vals.transpose(0, 1, 3, 2).reshape(g * 512, n)


B, S, D, DK, H = 2, 512, 1024, 1024, 8
DH = D // H
LN_EPS = 1e-8


def split_heads(x):
    return x.reshape(B, S, H, DH).transpose(0, 2, 1, 3).reshape(B * H, S, DH)


def merge_heads(x):
    return x.reshape(B, H, S, DH).transpose(0, 2, 1, 3).reshape(B, S, D)


def setup_inputs():
    s = mx_kscale(DK)
    keep = np.random.random((B, S, 1)) > 0.25
    q_relu = bf(np.maximum(np.random.standard_normal((B, S, D)) * 2.2, 0.0))
    k_relu = bf(np.maximum(np.random.standard_normal((B, S, D)) * 2.2, 0.0))
    keys = bf(np.random.standard_normal((B, S, DK)) * s)
    wv = np.random.standard_normal((D, DK)) * 2.2 / np.sqrt(DK) / s[None, :]
    Wv_words, Wv_scales = pack_weight(np.ascontiguousarray(wv.T), "e4m3")
    return {"q_relu": q_relu,
            "k_relu": k_relu,
            "keys": keys,
            "Wv_words": Wv_words,
            "Wv_scales": Wv_scales,
            "bv": bf(np.random.standard_normal(D) * 0.3),
            "queries": bf(np.random.standard_normal((B, S, D)) * keep),
            "ln_gamma": bf(1.0 + 0.1 * np.random.standard_normal(D)),
            "ln_beta": bf(0.1 * np.random.standard_normal(D))}


def reference(q_relu, k_relu, keys, Wv_words, Wv_scales, bv, queries, ln_gamma, ln_beta):
    x = f64(queries)
    v = np.maximum((mxq(f64(keys), 2, "e4m3") @ unpack_weight(Wv_words, Wv_scales, "e4m3")) + f64(bv), 0.0)
    q_, k_, v_ = split_heads(f64(q_relu)), split_heads(f64(k_relu)), split_heads(v)
    sc = q_ @ k_.transpose(0, 2, 1) / np.sqrt(DH)
    e = np.exp(sc - sc.max(-1, keepdims=True))
    mask = np.tile(np.where(np.abs(x).sum(-1, keepdims=True) > 0, 1.0, 0.0), (H, 1, 1))
    o = (mxq(e, 2, "e4m3") @ mxq(v_, 1, "e4m3")) / e.sum(-1, keepdims=True) * mask
    y = merge_heads(o) + x
    mu = y.mean(-1, keepdims=True)
    var = np.square(y - mu).mean(-1, keepdims=True)
    return (y - mu) / np.sqrt(var + LN_EPS) * f64(ln_gamma) + f64(ln_beta)

@@ -1,0 +1,322 @@
+import math
+from contextlib import ExitStack
+
+import concourse.mybir as mybir
+from concourse.masks import make_identity
+
+BF16 = mybir.dt.bfloat16
+F32 = mybir.dt.float32
+I32 = mybir.dt.int32
+U32 = mybir.dt.uint32
+U8 = mybir.dt.uint8
+FP8X4 = mybir.dt.float8_e4m3fn_x4
+ALU = mybir.AluOpType
+ACT = mybir.ActivationFunctionType
+AXIS_X = mybir.AxisListType.X
+
+P = 128
+PACK = 4
+B, S, D, H = 2, 512, 1024, 8
+DH = D // H
+TILES = S // P
+K_PASSES = D // (P * PACK)
+SCORE_SCALE = 1.0 / math.sqrt(DH)
+LN_EPS = 1e-8
+
+FLOPS = 2 * B * S * D * D + 2 * (2 * B * H * S * S * DH)
+
+
+def tile_multiheadattentionlayer_pa_kernel(
+    tc, q_relu, k_relu, keys, Wv_words, Wv_scales, bv, queries, ln_gamma, ln_beta, out
+):
+    nc = tc.nc
+    with ExitStack() as ctx:
+        keep = ctx.enter_context(tc.tile_pool(name="keep", bufs=1))
+        stage = ctx.enter_context(tc.tile_pool(name="stage", bufs=2))
+        work = ctx.enter_context(tc.tile_pool(name="work", bufs=3))
+        small = ctx.enter_context(tc.tile_pool(name="small", bufs=4))
+
+        ident_bf = keep.tile([P, P], BF16)
+        make_identity(nc, ident_bf[:])
+        ident_f32 = keep.tile([P, P], F32)
+        make_identity(nc, ident_f32[:])
+        neg_half = keep.tile([P, 1], F32)
+        nc.vector.memset(neg_half[:], -0.5)
+
+        w_scales = keep.tile([P, K_PASSES, D], U8, align_bytes=64)
+        nc.vector.memset(w_scales[:].rearrange("p g n -> p (g n)").bitcast(I32), 0)
+        for quad in range(4):
+            nc.sync.dma_start(
+                out=w_scales[32 * quad : 32 * quad + 4, :, :].bitcast(I32),
+                in_=Wv_scales[:, 4 * quad : 4 * quad + 4, :].rearrange("g r n -> r g n").bitcast(I32),
+            )
+
+        def load_tokens(name, src, b, order):
+            t = keep.tile([P, TILES, D], BF16, name=name + str(b))
+            if order == "words":
+                nc.sync.dma_start(
+                    out=t[:].rearrange("p (u e) d -> p u e d", u=2),
+                    in_=src[b].rearrange("(u p e) d -> p u e d", u=2, e=2),
+                )
+            elif order == "tiles":
+                nc.sync.dma_start(out=t[:], in_=src[b].rearrange("(j p) d -> p j d", j=TILES))
+            else:
+                nc.sync.dma_start(out=t[:], in_=src[b].rearrange("(p j) d -> p j d", j=TILES))
+            return t
+
+        bv_bc = keep.tile([P, D], BF16)
+        nc.scalar.dma_start(out=bv_bc[:], in_=bv.partition_broadcast(P))
+        gamma_bc = keep.tile([P, D], BF16)
+        nc.scalar.dma_start(out=gamma_bc[:], in_=ln_gamma.partition_broadcast(P))
+        beta_bc = keep.tile([P, D], BF16)
+        nc.scalar.dma_start(out=beta_bc[:], in_=ln_beta.partition_broadcast(P))
+
+        w_codes = keep.tile([P, K_PASSES, D], U32, align_bytes=64)
+        keys_sb = [load_tokens("keys_sb", keys, 0, "words")]
+        for g in range(K_PASSES):
+            nc.sync.dma_start(
+                out=w_codes[:, g, :].bitcast(I32),
+                in_=Wv_words[g].rearrange("p n t -> p (n t)").bitcast(I32),
+            )
+        k_sb = [load_tokens("k_sb", k_relu, 0, "tiles")]
+        q_sb = [load_tokens("q_sb", q_relu, 0, "rows")]
+        x_sb = [load_tokens("x_sb", queries, bb, "rows") for bb in range(B)]
+        keys_sb.append(load_tokens("keys_sb", keys, 1, "words"))
+        k_sb.append(load_tokens("k_sb", k_relu, 1, "tiles"))
+        q_sb.append(load_tokens("q_sb", q_relu, 1, "rows"))
+
+        qT = keep.tile([P, B, H, TILES, P], BF16)
+        kT = keep.tile([P, B, H, TILES, P], BF16)
+        keys_grouped = [
+            keep.tile([P, K_PASSES, S, PACK], BF16, align_bytes=64, name="keys_grouped" + str(b)) for b in range(B)
+        ]
+        keys_codes = keep.tile([P, K_PASSES, B, S], U32, align_bytes=64)
+        keys_scales = keep.tile([P, K_PASSES, B, S], U8, align_bytes=64)
+        v_codes = keep.tile([P, B, D], U32, align_bytes=64)
+        v_scales = keep.tile([P, B, D], U8, align_bytes=64)
+        abs_sum = keep.tile([P, TILES, B], F32)
+        mask01 = keep.tile([P, TILES, B], F32)
+
+        def transpose_heads(banks, src, dst, b, h0):
+            headsT = banks.tile([P, 2, TILES, P], BF16, tag="prep")
+            for i in range(2):
+                for j in range(TILES):
+                    nc.tensor.transpose(
+                        headsT[:, i, j, :], src[:, j, (h0 + i) * DH : (h0 + i + 1) * DH], ident_bf[:]
+                    )
+            nc.scalar.copy(out=dst[:, b, h0 : h0 + 2, :, :], in_=headsT[:])
+
+        def transpose_keys(banks, b, j):
+            keys_words = keys_sb[b][:, j, :].bitcast(F32)
+            keysT = banks.tile([P, K_PASSES, 2, P], F32, tag="prep")
+            for g in range(K_PASSES):
+                for u in range(2):
+                    nc.tensor.transpose(
+                        keysT[:, g, u, :], keys_words[:, 256 * g + u : 256 * (g + 1) : 2], ident_f32[:]
+                    )
+            nc.vector.tensor_copy(
+                out=keys_grouped[b][:].bitcast(F32)[:, :, j * P : (j + 1) * P, :],
+                in_=keysT[:].rearrange("p g u q -> p g q u"),
+            )
+
+        def quantise_keys(b):
+            for g in range(K_PASSES):
+                nc.vector.quantize_mx(
+                    out=keys_codes[:, g, b, :].bitcast(FP8X4),
+                    scales=keys_scales[:, g, b, :],
+                    in_=keys_grouped[b][:, g, :, :].rearrange("p q t -> p (q t)"),
+                )
+
+        def project_values(banks, b, h):
+            cols = slice(h * DH, (h + 1) * DH)
+            v_ps = banks.tile([P, TILES, DH], F32, tag="prep")
+            for j in range(TILES):
+                toks = slice(j * P, (j + 1) * P)
+                for g in range(K_PASSES):
+                    nc.tensor.matmul_mx(
+                        out=v_ps[:, j, :],
+                        lhsT=keys_codes[:, g, b, toks].bitcast(FP8X4),
+                        lhsT_scale=keys_scales[:, g, b, toks],
+                        rhs=w_codes[:, g, cols].bitcast(FP8X4),
+                        rhs_scale=w_scales[:, g, cols],
+                        start=(g == 0),
+                        stop=(g == K_PASSES - 1),
+                    )
+            v_grouped = stage.tile([P, DH, PACK], BF16, align_bytes=64)
+            nc.vector.tensor_tensor(
+                out=v_grouped[:],
+                in0=v_ps[:].rearrange("p j c -> p c j"),
+                in1=bv_bc[:, cols].unsqueeze(2).to_broadcast([P, DH, PACK]),
+                op=ALU.add,
+            )
+            v_flat = v_grouped[:].rearrange("p c j -> p (c j)")
+            nc.vector.tensor_scalar_max(v_flat, v_flat, 0.0)
+            nc.vector.quantize_mx(out=v_codes[:, b, cols].bitcast(FP8X4), scales=v_scales[:, b, cols], in_=v_flat)
+
+        def row_mask(j):
+            for bb in range(B):
+                abs_x = stage.tile([P, D], BF16)
+                nc.scalar.activation(
+                    out=abs_x[:], in_=x_sb[bb][:, j, :], func=ACT.Abs, accum_out=abs_sum[:, j, bb : bb + 1]
+                )
+            nc.vector.tensor_single_scalar(mask01[:, j, :], abs_sum[:, j, :], 0.0, op=ALU.is_gt)
+
+        with tc.psum_pool(name="psum_start", bufs=8) as banks:
+            for b in range(B):
+                for j in range(TILES):
+                    transpose_keys(banks, b, j)
+                quantise_keys(b)
+                for h0 in range(0, H, 2):
+                    transpose_heads(banks, k_sb[b], kT, b, h0)
+                    transpose_heads(banks, q_sb[b], qT, b, h0)
+                    project_values(banks, b, h0)
+                    project_values(banks, b, h0 + 1)
+                if b == 0:
+                    for j in range(TILES):
+                        row_mask(j)
+
+        psum_s = ctx.enter_context(tc.psum_pool(name="psum_s", bufs=4))
+        psum_t = ctx.enter_context(tc.psum_pool(name="psum_t", bufs=2))
+        psum_o = ctx.enter_context(tc.psum_pool(name="psum_o", bufs=2))
+
+        units = [(b, j, h) for b in range(B) for j in range(TILES) for h in range(H)]
+        n_pairs = len(units) // 2
+        scores, shifts, rowsums, es, eTs, e_groupeds, ys, statss = {}, {}, {}, {}, {}, {}, {}, {}
+        quantised = {}
+
+        def score(u):
+            b, j, h = units[u]
+            scores[u] = psum_s.tile([P, S], F32, name="s_ps")
+            nc.tensor.matmul(
+                scores[u][:],
+                lhsT=qT[:, b, h, j, :],
+                rhs=kT[:, b, h, :, :].rearrange("p t k -> p (t k)"),
+                start=True,
+                stop=True,
+            )
+
+        def row_max(pair):
+            rowmax = small.tile([P, 2], F32)
+            for i in range(2):
+                nc.vector.tensor_reduce(
+                    out=rowmax[:, i : i + 1], in_=scores[2 * pair + i][:], axis=AXIS_X, op=ALU.max
+                )
+            shifts[pair] = small.tile([P, 2], F32, name="shift")
+            nc.vector.tensor_scalar_mul(shifts[pair][:], rowmax[:], -SCORE_SCALE)
+
+        def exp_and_transpose(pair, i):
+            if i == 0:
+                es[pair] = work.tile([P, 2, S], BF16, name="e")
+                eTs[pair] = psum_t.tile([P, 2, 2, P], F32, name="eT")
+                rowsums[pair] = small.tile([P, 2], F32, name="rowsum")
+            nc.scalar.activation(
+                out=es[pair][:, i, :],
+                in_=scores[2 * pair + i][:],
+                func=ACT.Exp,
+                bias=shifts[pair][:, i : i + 1],
+                scale=SCORE_SCALE,
+                accum_out=rowsums[pair][:, i : i + 1],
+            )
+            e_words = es[pair][:, i, :].bitcast(F32)
+            for u in range(2):
+                nc.tensor.transpose(eTs[pair][:, i, u, :], e_words[:, u * P : (u + 1) * P], ident_f32[:])
+
+        def regroup(pair):
+            e_groupeds[pair] = work.tile([P, 2, P, PACK], BF16, align_bytes=64, name="e_grouped")
+            nc.scalar.copy(out=e_groupeds[pair][:].bitcast(F32), in_=eTs[pair][:].rearrange("p i u q -> p i q u"))
+
+        def quantise(pair):
+            e_codes = work.tile([P, 2 * P], U32, align_bytes=64)
+            e_scales = work.tile([P, 2 * P], U8, align_bytes=64)
+            nc.vector.quantize_mx(
+                out=e_codes[:].bitcast(FP8X4),
+                scales=e_scales[:],
+                in_=e_groupeds[pair][:].rearrange("p i q t -> p (i q t)"),
+            )
+            quantised[pair] = (e_codes, e_scales)
+
+        def multiply(pair):
+            b, j, h0 = units[2 * pair]
+            e_codes, e_scales = quantised[pair]
+            o_ps = psum_o.tile([P, 2, DH], F32)
+            outputs[pair] = o_ps
+            for i in range(2):
+                cols = slice((h0 + i) * DH, (h0 + i + 1) * DH)
+                nc.tensor.matmul_mx(
+                    out=o_ps[:, i, :],
+                    lhsT=e_codes[:, i * P : (i + 1) * P].bitcast(FP8X4),
+                    lhsT_scale=e_scales[:, i * P : (i + 1) * P],
+                    rhs=v_codes[:, b, cols].bitcast(FP8X4),
+                    rhs_scale=v_scales[:, b, cols],
+                    start=True,
+                    stop=True,
+                )
+
+        def residual(pair):
+            b, j, h0 = units[2 * pair]
+            o_ps = outputs[pair]
+            if h0 == 0:
+                ys[(b, j)] = work.tile([P, D], F32, name="y")
+                statss[(b, j)] = small.tile([P, H // 2, 6], F32, name="stats")
+            y = ys[(b, j)]
+            recip = small.tile([P, 2], F32)
+            nc.vector.reciprocal(recip[:], rowsums[pair][:])
+            gain = small.tile([P, 2], F32)
+            nc.vector.tensor_tensor(out=gain[:], in0=recip[:], in1=mask01[:, j, :], op=ALU.mult)
+            for i in range(2):
+                cols = slice((h0 + i) * DH, (h0 + i + 1) * DH)
+                nc.vector.scalar_tensor_tensor(
+                    out=y[:, cols],
+                    in0=o_ps[:, i, :],
+                    scalar=gain[:, i : i + 1],
+                    in1=x_sb[b][:, j, cols],
+                    op0=ALU.mult,
+                    op1=ALU.add,
+                )
+            nc.vector.bn_stats(out=statss[(b, j)][:, h0 // 2, :], in_=y[:, h0 * DH : (h0 + 2) * DH])
+            if h0 == H - 2:
+                layer_norm(b, j)
+
+        def layer_norm(b, j):
+            y = ys[(b, j)]
+            mean_var = small.tile([P, 2], F32)
+            nc.vector.bn_aggr(out=mean_var[:], in_=statss[(b, j)][:].rearrange("p c s -> p (c s)"))
+            neg_mean = small.tile([P, 1], F32)
+            nc.gpsimd.tensor_scalar(neg_mean[:], mean_var[:, 0:1], -1.0, 0.0, op0=ALU.mult, op1=ALU.add)
+            var_eps = small.tile([P, 1], F32)
+            nc.gpsimd.tensor_scalar(var_eps[:], mean_var[:, 1:2], 1.0, LN_EPS, op0=ALU.mult, op1=ALU.add)
+            rstd = small.tile([P, 1], F32)
+            nc.gpsimd.tensor_tensor(out=rstd[:], in0=var_eps[:], in1=neg_half[:], op=ALU.pow)
+            if (b, j) == (B - 1, TILES - 1):
+                nc.vector.scalar_tensor_tensor(
+                    out=y[:], in0=y[:], scalar=neg_mean[:], in1=gamma_bc[:], op0=ALU.add, op1=ALU.mult
+                )
+                nc.vector.scalar_tensor_tensor(
+                    out=y[:], in0=y[:], scalar=rstd[:], in1=beta_bc[:], op0=ALU.mult, op1=ALU.add
+                )
+            else:
+                nc.gpsimd.tensor_scalar(y[:], y[:], neg_mean[:], rstd[:], op0=ALU.add, op1=ALU.mult)
+                nc.gpsimd.tensor_tensor(out=y[:], in0=y[:], in1=gamma_bc[:], op=ALU.mult)
+                nc.gpsimd.tensor_tensor(out=y[:], in0=y[:], in1=beta_bc[:], op=ALU.add)
+            nc.sync.dma_start(out=out[b].rearrange("(p j) d -> p j d", j=TILES)[:, j, :], in_=y[:])
+
+        outputs = {}
+        for u in range(4):
+            score(u)
+        row_max(0)
+        for s in range(n_pairs + 3):
+            if 2 <= s < n_pairs + 2:
+                quantise(s - 2)
+            if s + 1 < n_pairs:
+                row_max(s + 1)
+            if s < n_pairs:
+                for i in range(2):
+                    exp_and_transpose(s, i)
+                    if 2 * s + 4 + i < len(units):
+                        score(2 * s + 4 + i)
+            if 1 <= s < n_pairs + 1:
+                regroup(s - 1)
+            if 2 <= s < n_pairs + 2:
+                multiply(s - 2)
+            if s >= 3:
+                residual(s - 3)

@@ -181,7 +181,7 @@ def tile_multiheadattentionlayer_pa_kernel(
 
         units = [(b, j, h) for b in range(B) for j in range(TILES) for h in range(H)]
         n_pairs = len(units) // 2
-        scores, shifts, rowsums, es, eTs, e_groupeds, ys, statss = {}, {}, {}, {}, {}, {}, {}, {}
+        scores, shifts, rowsums, es, eTs, e_groupeds, ys = {}, {}, {}, {}, {}, {}, {}
         quantised = {}
 
         def score(u):
@@ -257,7 +257,6 @@ def tile_multiheadattentionlayer_pa_kernel(
             o_ps = outputs[pair]
             if h0 == 0:
                 ys[(b, j)] = work.tile([P, D], F32, name="y")
-                statss[(b, j)] = small.tile([P, H // 2, 6], F32, name="stats")
             y = ys[(b, j)]
             recip = small.tile([P, 2], F32)
             nc.vector.reciprocal(recip[:], rowsums[pair][:])
@@ -273,32 +272,32 @@ def tile_multiheadattentionlayer_pa_kernel(
                     op0=ALU.mult,
                     op1=ALU.add,
                 )
-            nc.vector.bn_stats(out=statss[(b, j)][:, h0 // 2, :], in_=y[:, h0 * DH : (h0 + 2) * DH])
             if h0 == H - 2:
                 layer_norm(b, j)
 
         def layer_norm(b, j):
             y = ys[(b, j)]
-            mean_var = small.tile([P, 2], F32)
-            nc.vector.bn_aggr(out=mean_var[:], in_=statss[(b, j)][:].rearrange("p c s -> p (c s)"))
+            squares = stage.tile([P, D], BF16, name="unused")
+            y_sum = small.tile([P, 1], F32)
+            nc.scalar.activation(out=squares[:], in_=y[:], func=ACT.Identity, accum_out=y_sum[:])
             neg_mean = small.tile([P, 1], F32)
-            nc.gpsimd.tensor_scalar(neg_mean[:], mean_var[:, 0:1], -1.0, 0.0, op0=ALU.mult, op1=ALU.add)
+            nc.scalar.mul(neg_mean[:], y_sum[:], -1.0 / D)
+            dev_sum = small.tile([P, 1], F32)
+            nc.scalar.activation(
+                out=squares[:], in_=y[:], func=ACT.Square, bias=neg_mean[:], accum_out=dev_sum[:]
+            )
             var_eps = small.tile([P, 1], F32)
-            nc.gpsimd.tensor_scalar(var_eps[:], mean_var[:, 1:2], 1.0, LN_EPS, op0=ALU.mult, op1=ALU.add)
+            nc.gpsimd.tensor_scalar(var_eps[:], dev_sum[:], 1.0 / D, LN_EPS, op0=ALU.mult, op1=ALU.add)
             rstd = small.tile([P, 1], F32)
             nc.gpsimd.tensor_tensor(out=rstd[:], in0=var_eps[:], in1=neg_half[:], op=ALU.pow)
-            if (b, j) == (B - 1, TILES - 1):
-                nc.vector.scalar_tensor_tensor(
-                    out=y[:], in0=y[:], scalar=neg_mean[:], in1=gamma_bc[:], op0=ALU.add, op1=ALU.mult
-                )
-                nc.vector.scalar_tensor_tensor(
-                    out=y[:], in0=y[:], scalar=rstd[:], in1=beta_bc[:], op0=ALU.mult, op1=ALU.add
-                )
-            else:
-                nc.gpsimd.tensor_scalar(y[:], y[:], neg_mean[:], rstd[:], op0=ALU.add, op1=ALU.mult)
-                nc.gpsimd.tensor_tensor(out=y[:], in0=y[:], in1=gamma_bc[:], op=ALU.mult)
-                nc.gpsimd.tensor_tensor(out=y[:], in0=y[:], in1=beta_bc[:], op=ALU.add)
-            nc.sync.dma_start(out=out[b].rearrange("(p j) d -> p j d", j=TILES)[:, j, :], in_=y[:])
+            normed = work.tile([P, D], F32)
+            nc.vector.scalar_tensor_tensor(
+                out=normed[:], in0=y[:], scalar=neg_mean[:], in1=gamma_bc[:], op0=ALU.add, op1=ALU.mult
+            )
+            nc.vector.scalar_tensor_tensor(
+                out=normed[:], in0=normed[:], scalar=rstd[:], in1=beta_bc[:], op0=ALU.mult, op1=ALU.add
+            )
+            nc.sync.dma_start(out=out[b].rearrange("(p j) d -> p j d", j=TILES)[:, j, :], in_=normed[:])
 
         outputs = {}
         for u in range(4):

@@ -181,8 +181,10 @@ def tile_multiheadattentionlayer_pa_kernel(
 
         units = [(b, j, h) for b in range(B) for j in range(TILES) for h in range(H)]
         n_pairs = len(units) // 2
-        scores, shifts, rowsums, es, eTs, e_groupeds, ys = {}, {}, {}, {}, {}, {}, {}
-        quantised = {}
+        n_tiles = n_pairs // 4
+        HALF = D // 2
+        scores, rowmaxs, shifts, rowsums, es, eTs, e_groupeds, quantised, outputs = {}, {}, {}, {}, {}, {}, {}, {}, {}
+        recips, gains, ys, sums, neg_means, rstds, normeds = {}, {}, {}, {}, {}, {}, {}
 
         def score(u):
             b, j, h = units[u]
@@ -195,19 +197,20 @@ def tile_multiheadattentionlayer_pa_kernel(
                 stop=True,
             )
 
-        def row_max(pair):
-            rowmax = small.tile([P, 2], F32)
-            for i in range(2):
-                nc.vector.tensor_reduce(
-                    out=rowmax[:, i : i + 1], in_=scores[2 * pair + i][:], axis=AXIS_X, op=ALU.max
-                )
-            shifts[pair] = small.tile([P, 2], F32, name="shift")
-            nc.vector.tensor_scalar_mul(shifts[pair][:], rowmax[:], -SCORE_SCALE)
+        def row_max(pair, i):
+            if i == 0:
+                rowmaxs[pair] = small.tile([P, 2], F32, name="rowmax")
+            nc.vector.tensor_reduce(
+                out=rowmaxs[pair][:, i : i + 1], in_=scores[2 * pair + i][:], axis=AXIS_X, op=ALU.max
+            )
 
-        def exp_and_transpose(pair, i):
+        def shift_of(pair):
+            shifts[pair] = small.tile([P, 2], F32, name="shift")
+            nc.vector.tensor_scalar_mul(shifts[pair][:], rowmaxs[pair][:], -SCORE_SCALE)
+
+        def exponentiate(pair, i):
             if i == 0:
                 es[pair] = work.tile([P, 2, S], BF16, name="e")
-                eTs[pair] = psum_t.tile([P, 2, 2, P], F32, name="eT")
                 rowsums[pair] = small.tile([P, 2], F32, name="rowsum")
             nc.scalar.activation(
                 out=es[pair][:, i, :],
@@ -217,6 +220,10 @@ def tile_multiheadattentionlayer_pa_kernel(
                 scale=SCORE_SCALE,
                 accum_out=rowsums[pair][:, i : i + 1],
             )
+
+        def transpose_e(pair, i):
+            if i == 0:
+                eTs[pair] = psum_t.tile([P, 2, 2, P], F32, name="eT")
             e_words = es[pair][:, i, :].bitcast(F32)
             for u in range(2):
                 nc.tensor.transpose(eTs[pair][:, i, u, :], e_words[:, u * P : (u + 1) * P], ident_f32[:])
@@ -238,12 +245,11 @@ def tile_multiheadattentionlayer_pa_kernel(
         def multiply(pair):
             b, j, h0 = units[2 * pair]
             e_codes, e_scales = quantised[pair]
-            o_ps = psum_o.tile([P, 2, DH], F32)
-            outputs[pair] = o_ps
+            outputs[pair] = psum_o.tile([P, 2, DH], F32, name="o_ps")
             for i in range(2):
                 cols = slice((h0 + i) * DH, (h0 + i + 1) * DH)
                 nc.tensor.matmul_mx(
-                    out=o_ps[:, i, :],
+                    out=outputs[pair][:, i, :],
                     lhsT=e_codes[:, i * P : (i + 1) * P].bitcast(FP8X4),
                     lhsT_scale=e_scales[:, i * P : (i + 1) * P],
                     rhs=v_codes[:, b, cols].bitcast(FP8X4),
@@ -252,70 +258,142 @@ def tile_multiheadattentionlayer_pa_kernel(
                     stop=True,
                 )
 
-        def residual(pair):
-            b, j, h0 = units[2 * pair]
-            o_ps = outputs[pair]
-            if h0 == 0:
-                ys[(b, j)] = work.tile([P, D], F32, name="y")
-            y = ys[(b, j)]
-            recip = small.tile([P, 2], F32)
-            nc.vector.reciprocal(recip[:], rowsums[pair][:])
-            gain = small.tile([P, 2], F32)
-            nc.vector.tensor_tensor(out=gain[:], in0=recip[:], in1=mask01[:, j, :], op=ALU.mult)
-            for i in range(2):
-                cols = slice((h0 + i) * DH, (h0 + i + 1) * DH)
-                nc.vector.scalar_tensor_tensor(
-                    out=y[:, cols],
-                    in0=o_ps[:, i, :],
-                    scalar=gain[:, i : i + 1],
-                    in1=x_sb[b][:, j, cols],
-                    op0=ALU.mult,
-                    op1=ALU.add,
-                )
-            if h0 == H - 2:
-                layer_norm(b, j)
+        def reciprocal_of(pair):
+            recips[pair] = small.tile([P, 2], F32, name="recip")
+            nc.vector.reciprocal(recips[pair][:], rowsums[pair][:])
 
-        def layer_norm(b, j):
-            y = ys[(b, j)]
-            squares = stage.tile([P, D], BF16, name="unused")
-            y_sum = small.tile([P, 1], F32)
-            nc.scalar.activation(out=squares[:], in_=y[:], func=ACT.Identity, accum_out=y_sum[:])
-            neg_mean = small.tile([P, 1], F32)
-            nc.scalar.mul(neg_mean[:], y_sum[:], -1.0 / D)
-            dev_sum = small.tile([P, 1], F32)
-            nc.scalar.activation(
-                out=squares[:], in_=y[:], func=ACT.Square, bias=neg_mean[:], accum_out=dev_sum[:]
+        def gain_of(pair):
+            j = units[2 * pair][1]
+            gains[pair] = small.tile([P, 2], F32, name="gain")
+            nc.vector.tensor_tensor(out=gains[pair][:], in0=recips[pair][:], in1=mask01[:, j, :], op=ALU.mult)
+
+        def residual(pair, i):
+            b, j, h0 = units[2 * pair]
+            if h0 == 0 and i == 0:
+                ys[pair // 4] = work.tile([P, D], F32, name="y")
+            cols = slice((h0 + i) * DH, (h0 + i + 1) * DH)
+            nc.vector.scalar_tensor_tensor(
+                out=ys[pair // 4][:, cols],
+                in0=outputs[pair][:, i, :],
+                scalar=gains[pair][:, i : i + 1],
+                in1=x_sb[b][:, j, cols],
+                op0=ALU.mult,
+                op1=ALU.add,
             )
+
+        def sum_y(tile_no, half):
+            if half == 0:
+                sums[tile_no] = small.tile([P, 4], F32, name="sums")
+            unused = stage.tile([P, HALF], BF16, name="unused")
+            nc.scalar.activation(
+                out=unused[:],
+                in_=ys[tile_no][:, half * HALF : (half + 1) * HALF],
+                func=ACT.Identity,
+                accum_out=sums[tile_no][:, half : half + 1],
+            )
+
+        def mean_of(tile_no):
+            unused = small.tile([P, 2], F32, name="unused2")
+            neg_means[tile_no] = small.tile([P, 1], F32, name="neg_mean")
+            nc.scalar.activation(
+                out=unused[:], in_=sums[tile_no][:, 0:2], func=ACT.Identity, scale=-1.0 / D, accum_out=neg_means[tile_no][:]
+            )
+
+        def sum_squares(tile_no, half):
+            unused = stage.tile([P, HALF], BF16, name="unused")
+            nc.scalar.activation(
+                out=unused[:],
+                in_=ys[tile_no][:, half * HALF : (half + 1) * HALF],
+                func=ACT.Square,
+                bias=neg_means[tile_no][:],
+                accum_out=sums[tile_no][:, 2 + half : 3 + half],
+            )
+
+        def rstd_of(tile_no):
+            dev_sum = small.tile([P, 1], F32)
+            nc.gpsimd.tensor_tensor(out=dev_sum[:], in0=sums[tile_no][:, 2:3], in1=sums[tile_no][:, 3:4], op=ALU.add)
             var_eps = small.tile([P, 1], F32)
             nc.gpsimd.tensor_scalar(var_eps[:], dev_sum[:], 1.0 / D, LN_EPS, op0=ALU.mult, op1=ALU.add)
-            rstd = small.tile([P, 1], F32)
-            nc.gpsimd.tensor_tensor(out=rstd[:], in0=var_eps[:], in1=neg_half[:], op=ALU.pow)
-            normed = work.tile([P, D], F32)
-            nc.vector.scalar_tensor_tensor(
-                out=normed[:], in0=y[:], scalar=neg_mean[:], in1=gamma_bc[:], op0=ALU.add, op1=ALU.mult
-            )
-            nc.vector.scalar_tensor_tensor(
-                out=normed[:], in0=normed[:], scalar=rstd[:], in1=beta_bc[:], op0=ALU.mult, op1=ALU.add
-            )
-            nc.sync.dma_start(out=out[b].rearrange("(p j) d -> p j d", j=TILES)[:, j, :], in_=normed[:])
+            rstds[tile_no] = small.tile([P, 1], F32, name="rstd")
+            nc.gpsimd.tensor_tensor(out=rstds[tile_no][:], in0=var_eps[:], in1=neg_half[:], op=ALU.pow)
 
-        outputs = {}
-        for u in range(4):
-            score(u)
-        row_max(0)
-        for s in range(n_pairs + 3):
-            if 2 <= s < n_pairs + 2:
-                quantise(s - 2)
-            if s + 1 < n_pairs:
-                row_max(s + 1)
-            if s < n_pairs:
-                for i in range(2):
-                    exp_and_transpose(s, i)
-                    if 2 * s + 4 + i < len(units):
-                        score(2 * s + 4 + i)
-            if 1 <= s < n_pairs + 1:
-                regroup(s - 1)
-            if 2 <= s < n_pairs + 2:
-                multiply(s - 2)
-            if s >= 3:
-                residual(s - 3)
+        def centre(tile_no, half):
+            if half == 0:
+                normeds[tile_no] = work.tile([P, D], F32, name="normed")
+            cols = slice(half * HALF, (half + 1) * HALF)
+            nc.vector.scalar_tensor_tensor(
+                out=normeds[tile_no][:, cols],
+                in0=ys[tile_no][:, cols],
+                scalar=neg_means[tile_no][:],
+                in1=gamma_bc[:, cols],
+                op0=ALU.add,
+                op1=ALU.mult,
+            )
+
+        def scale_and_store(tile_no, half):
+            b, j = tile_no // TILES, tile_no % TILES
+            cols = slice(half * HALF, (half + 1) * HALF)
+            nc.vector.scalar_tensor_tensor(
+                out=normeds[tile_no][:, cols],
+                in0=normeds[tile_no][:, cols],
+                scalar=rstds[tile_no][:],
+                in1=beta_bc[:, cols],
+                op0=ALU.mult,
+                op1=ALU.add,
+            )
+            nc.sync.dma_start(
+                out=out[b].rearrange("(p j) d -> p j d", j=TILES)[:, j, cols], in_=normeds[tile_no][:, cols]
+            )
+
+        with tc.manual_schedule():
+            for u in range(4):
+                score(u)
+            row_max(0, 0)
+            row_max(0, 1)
+            shift_of(0)
+            for s in range(n_pairs + 9):
+                stats_tile, stats_piece = divmod(s - 7, 4)
+                apply_tile, apply_piece = divmod(s - 9, 4)
+                finishing = 0 <= s - 3 < n_pairs
+                ahead = s + 1 < n_pairs
+
+                if 0 <= stats_tile < n_tiles and stats_piece == 2:
+                    mean_of(stats_tile)
+                if finishing:
+                    multiply(s - 3)
+                    reciprocal_of(s - 3)
+                if ahead:
+                    row_max(s + 1, 0)
+                if finishing:
+                    gain_of(s - 3)
+                if ahead:
+                    row_max(s + 1, 1)
+                if finishing:
+                    residual(s - 3, 0)
+                if ahead:
+                    shift_of(s + 1)
+                if finishing:
+                    residual(s - 3, 1)
+                if 0 <= apply_tile < n_tiles:
+                    if apply_piece < 2:
+                        centre(apply_tile, apply_piece)
+                    else:
+                        scale_and_store(apply_tile, apply_piece - 2)
+                if 0 <= s - 2 < n_pairs:
+                    quantise(s - 2)
+
+                if s < n_pairs:
+                    for i in range(2):
+                        exponentiate(s, i)
+                        transpose_e(s, i)
+                        if 2 * (s + 2) + i < len(units):
+                            score(2 * (s + 2) + i)
+                if 0 <= s - 1 < n_pairs:
+                    regroup(s - 1)
+                if 0 <= stats_tile < n_tiles:
+                    if stats_piece < 2:
+                        sum_y(stats_tile, stats_piece)
+                    else:
+                        sum_squares(stats_tile, stats_piece - 2)
+                    if stats_piece == 3:
+                        rstd_of(stats_tile)

@@ -64,12 +64,11 @@ def tile_multiheadattentionlayer_pa_kernel(
                 nc.sync.dma_start(out=t[:], in_=src[b].rearrange("(p j) d -> p j d", j=TILES))
             return t
 
-        bv_bc = keep.tile([P, D], BF16)
-        nc.scalar.dma_start(out=bv_bc[:], in_=bv.partition_broadcast(P))
-        gamma_bc = keep.tile([P, D], BF16)
-        nc.scalar.dma_start(out=gamma_bc[:], in_=ln_gamma.partition_broadcast(P))
-        beta_bc = keep.tile([P, D], BF16)
-        nc.scalar.dma_start(out=beta_bc[:], in_=ln_beta.partition_broadcast(P))
+        ones = keep.tile([P, P], BF16)
+        nc.vector.memset(ones[:], 1.0)
+        bv_row = keep.tile([P, D], BF16)
+        nc.vector.memset(bv_row[:], 0.0)
+        nc.sync.dma_start(out=bv_row[0:1, :], in_=bv.rearrange("(o n) -> o n", o=1))
 
         w_codes = keep.tile([P, K_PASSES, D], U32, align_bytes=64)
         keys_sb = [load_tokens("keys_sb", keys, 0, "words")]
@@ -80,10 +79,14 @@ def tile_multiheadattentionlayer_pa_kernel(
             )
         k_sb = [load_tokens("k_sb", k_relu, 0, "tiles")]
         q_sb = [load_tokens("q_sb", q_relu, 0, "rows")]
-        x_sb = [load_tokens("x_sb", queries, bb, "rows") for bb in range(B)]
         keys_sb.append(load_tokens("keys_sb", keys, 1, "words"))
         k_sb.append(load_tokens("k_sb", k_relu, 1, "tiles"))
         q_sb.append(load_tokens("q_sb", q_relu, 1, "rows"))
+        x_sb = [load_tokens("x_sb", queries, bb, "rows") for bb in range(B)]
+        gamma_bc = keep.tile([P, D], BF16)
+        nc.sync.dma_start(out=gamma_bc[:], in_=ln_gamma.partition_broadcast(P))
+        beta_bc = keep.tile([P, D], BF16)
+        nc.sync.dma_start(out=beta_bc[:], in_=ln_beta.partition_broadcast(P))
 
         qT = keep.tile([P, B, H, TILES, P], BF16)
         kT = keep.tile([P, B, H, TILES, P], BF16)
@@ -162,6 +165,12 @@ def tile_multiheadattentionlayer_pa_kernel(
             nc.vector.tensor_single_scalar(mask01[:, j, :], abs_sum[:, j, :], 0.0, op=ALU.is_gt)
 
         with tc.psum_pool(name="psum_start", bufs=8) as banks:
+            bv_bc = keep.tile([P, D], BF16)
+            for c in range(D // S):
+                cols = slice(c * S, (c + 1) * S)
+                bv_ps = banks.tile([P, S], F32, tag="prep")
+                nc.tensor.matmul(bv_ps[:], lhsT=ones[:], rhs=bv_row[:, cols], start=True, stop=True)
+                nc.scalar.copy(out=bv_bc[:, cols], in_=bv_ps[:])
             for b in range(B):
                 for j in range(TILES):
                     transpose_keys(banks, b, j)
@@ -171,9 +180,8 @@ def tile_multiheadattentionlayer_pa_kernel(
                     transpose_heads(banks, q_sb[b], qT, b, h0)
                     project_values(banks, b, h0)
                     project_values(banks, b, h0 + 1)
-                if b == 0:
-                    for j in range(TILES):
-                        row_mask(j)
+            for j in range(TILES):
+                row_mask(j)
 
         psum_s = ctx.enter_context(tc.psum_pool(name="psum_s", bufs=4))
         psum_t = ctx.enter_context(tc.psum_pool(name="psum_t", bufs=2))

@@ -42,6 +42,8 @@ def tile_multiheadattentionlayer_pa_kernel(
         make_identity(nc, ident_f32[:])
         neg_half = keep.tile([P, 1], F32)
         nc.vector.memset(neg_half[:], -0.5)
+        neg_one = keep.tile([P, 2], F32)
+        nc.vector.memset(neg_one[:], -1.0)
 
         w_scales = keep.tile([P, K_PASSES, D], U8, align_bytes=64)
         nc.vector.memset(w_scales[:].rearrange("p g n -> p (g n)").bitcast(I32), 0)
@@ -268,12 +270,12 @@ def tile_multiheadattentionlayer_pa_kernel(
 
         def reciprocal_of(pair):
             recips[pair] = small.tile([P, 2], F32, name="recip")
-            nc.vector.reciprocal(recips[pair][:], rowsums[pair][:])
+            nc.gpsimd.tensor_tensor(out=recips[pair][:], in0=rowsums[pair][:], in1=neg_one[:], op=ALU.pow)
 
         def gain_of(pair):
             j = units[2 * pair][1]
             gains[pair] = small.tile([P, 2], F32, name="gain")
-            nc.vector.tensor_tensor(out=gains[pair][:], in0=recips[pair][:], in1=mask01[:, j, :], op=ALU.mult)
+            nc.gpsimd.tensor_tensor(out=gains[pair][:], in0=recips[pair][:], in1=mask01[:, j, :], op=ALU.mult)
 
         def residual(pair, i):
             b, j, h0 = units[2 * pair]
@@ -318,10 +320,11 @@ def tile_multiheadattentionlayer_pa_kernel(
             )
 
         def rstd_of(tile_no):
-            dev_sum = small.tile([P, 1], F32)
-            nc.gpsimd.tensor_tensor(out=dev_sum[:], in0=sums[tile_no][:, 2:3], in1=sums[tile_no][:, 3:4], op=ALU.add)
+            unused = small.tile([P, 2], F32, name="unused2")
             var_eps = small.tile([P, 1], F32)
-            nc.gpsimd.tensor_scalar(var_eps[:], dev_sum[:], 1.0 / D, LN_EPS, op0=ALU.mult, op1=ALU.add)
+            nc.scalar.activation(
+                out=unused[:], in_=sums[tile_no][:, 2:4], func=ACT.Identity, scale=1.0 / D, bias=LN_EPS / 2, accum_out=var_eps[:]
+            )
             rstds[tile_no] = small.tile([P, 1], F32, name="rstd")
             nc.gpsimd.tensor_tensor(out=rstds[tile_no][:], in0=var_eps[:], in1=neg_half[:], op=ALU.pow)
 
@@ -359,22 +362,19 @@ def tile_multiheadattentionlayer_pa_kernel(
             row_max(0, 0)
             row_max(0, 1)
             shift_of(0)
-            for s in range(n_pairs + 9):
-                stats_tile, stats_piece = divmod(s - 7, 4)
+            for s in range(n_pairs + 10):
+                stats_tile, stats_piece = divmod(s - 6, 4)
                 apply_tile, apply_piece = divmod(s - 9, 4)
+                multiplying = 0 <= s - 2 < n_pairs
                 finishing = 0 <= s - 3 < n_pairs
                 ahead = s + 1 < n_pairs
 
-                if 0 <= stats_tile < n_tiles and stats_piece == 2:
-                    mean_of(stats_tile)
-                if finishing:
-                    multiply(s - 3)
-                    reciprocal_of(s - 3)
+                if multiplying:
+                    reciprocal_of(s - 2)
+                    gain_of(s - 2)
+                    quantise(s - 2)
                 if ahead:
                     row_max(s + 1, 0)
-                if finishing:
-                    gain_of(s - 3)
-                if ahead:
                     row_max(s + 1, 1)
                 if finishing:
                     residual(s - 3, 0)
@@ -382,20 +382,20 @@ def tile_multiheadattentionlayer_pa_kernel(
                     shift_of(s + 1)
                 if finishing:
                     residual(s - 3, 1)
-                if 0 <= apply_tile < n_tiles:
-                    if apply_piece < 2:
-                        centre(apply_tile, apply_piece)
-                    else:
-                        scale_and_store(apply_tile, apply_piece - 2)
-                if 0 <= s - 2 < n_pairs:
-                    quantise(s - 2)
 
-                if s < n_pairs:
-                    for i in range(2):
+                for i in range(2):
+                    if s < n_pairs:
                         exponentiate(s, i)
                         transpose_e(s, i)
-                        if 2 * (s + 2) + i < len(units):
-                            score(2 * (s + 2) + i)
+                    if 2 * (s + 2) + i < len(units):
+                        score(2 * (s + 2) + i)
+                    if i == 0:
+                        if multiplying:
+                            multiply(s - 2)
+                        if 0 <= stats_tile < n_tiles and stats_piece == 2:
+                            mean_of(stats_tile)
+                        if 0 <= stats_tile - 1 < n_tiles and stats_piece == 0:
+                            rstd_of(stats_tile - 1)
                 if 0 <= s - 1 < n_pairs:
                     regroup(s - 1)
                 if 0 <= stats_tile < n_tiles:
@@ -403,5 +403,9 @@ def tile_multiheadattentionlayer_pa_kernel(
                         sum_y(stats_tile, stats_piece)
                     else:
                         sum_squares(stats_tile, stats_piece - 2)
-                    if stats_piece == 3:
-                        rstd_of(stats_tile)
+
+                if 0 <= apply_tile < n_tiles:
+                    if apply_piece < 2:
+                        centre(apply_tile, apply_piece)
+                    else:
+                        scale_and_store(apply_tile, apply_piece - 2)

@@ -22,6 +22,7 @@ TILES = S // P
 K_PASSES = D // (P * PACK)
 SCORE_SCALE = 1.0 / math.sqrt(DH)
 LN_EPS = 1e-8
+BF16_MAX = 255.0 * 2.0**120
 
 FLOPS = 2 * B * S * D * D + 2 * (2 * B * H * S * S * DH)
 
@@ -32,63 +33,85 @@ def tile_multiheadattentionlayer_pa_kernel(
     nc = tc.nc
     with ExitStack() as ctx:
         keep = ctx.enter_context(tc.tile_pool(name="keep", bufs=1))
-        stage = ctx.enter_context(tc.tile_pool(name="stage", bufs=2))
+        stage = ctx.enter_context(tc.tile_pool(name="stage", bufs=3))
         work = ctx.enter_context(tc.tile_pool(name="work", bufs=3))
-        small = ctx.enter_context(tc.tile_pool(name="small", bufs=4))
+        rows = ctx.enter_context(tc.tile_pool(name="rows", bufs=6))
+        small = ctx.enter_context(tc.tile_pool(name="small", bufs=6))
+        psum_s = ctx.enter_context(tc.psum_pool(name="psum_s", bufs=4))
+        psum_t = ctx.enter_context(tc.psum_pool(name="psum_t", bufs=1))
+        psum_o = ctx.enter_context(tc.psum_pool(name="psum_o", bufs=1))
+        psum_p = ctx.enter_context(tc.psum_pool(name="psum_p", bufs=2))
+        ctx.enter_context(tc.manual_schedule())
+
+        HALF = D // 2
+        k_sb = [keep.tile([P, TILES, D], BF16, name="k_sb" + str(b)) for b in range(B)]
+        q_sb = [keep.tile([P, TILES, D], BF16, name="q_sb" + str(b)) for b in range(B)]
+        x_sb = [keep.tile([P, TILES, D], BF16, name="x_sb" + str(b)) for b in range(B)]
+        keys_sb = [keep.tile([P, TILES, D], BF16, name="keys_sb" + str(b)) for b in range(B)]
+        w_scales = keep.tile([P, K_PASSES, D], U8, align_bytes=64)
+        w_codes = keep.tile([P, K_PASSES, D], U32, align_bytes=64)
+        bv_row = keep.tile([P, D], BF16)
+        gamma_bc = keep.tile([P, D], BF16)
+        beta_bc = keep.tile([P, D], BF16)
+
+        def load_k(b, cols):
+            nc.sync.dma_start(out=k_sb[b][:, :, cols], in_=k_relu[b].rearrange("(j p) d -> p j d", j=TILES)[:, :, cols])
+
+        def load_q(b, cols):
+            nc.sync.dma_start(out=q_sb[b][:, :, cols], in_=q_relu[b].rearrange("(p j) d -> p j d", j=TILES)[:, :, cols])
+
+        def load_x(b, slots):
+            nc.sync.dma_start(out=x_sb[b][:, slots, :], in_=queries[b].rearrange("(p j) d -> p j d", j=TILES)[:, slots, :])
+
+        def load_keys(b):
+            for u in range(2):
+                nc.sync.dma_start(
+                    out=keys_sb[b][:, 2 * u : 2 * u + 2, :],
+                    in_=keys[b].rearrange("(u p e) d -> p u e d", u=2, e=2)[:, u, :, :],
+                )
+
+        nc.vector.memset(bv_row[:], 0.0)
+        nc.vector.memset(w_scales[:].rearrange("p g n -> p (g n)").bitcast(I32), 0)
+
+        load_k(0, slice(0, HALF // 2))
+        load_q(0, slice(0, HALF // 2))
+        nc.sync.dma_start(out=bv_row[0:1, :], in_=bv.rearrange("(o n) -> o n", o=1))
+        load_k(0, slice(HALF // 2, HALF))
+        load_q(0, slice(HALF // 2, HALF))
+        load_keys(0)
+        for quad in range(4):
+            nc.sync.dma_start(
+                out=w_scales[32 * quad : 32 * quad + 4, :, :].bitcast(I32),
+                in_=Wv_scales[:, 4 * quad : 4 * quad + 4, :].rearrange("g r n -> r g n").bitcast(I32),
+            )
+        for g in range(K_PASSES):
+            nc.sync.dma_start(
+                out=w_codes[:, g, :].bitcast(I32),
+                in_=Wv_words[g].rearrange("p n t -> p (n t)").bitcast(I32),
+            )
+        for slots in (slice(0, 2), slice(2, 4)):
+            for b in range(B):
+                load_x(b, slots)
+        load_k(0, slice(HALF, D))
+        load_q(0, slice(HALF, D))
+        load_keys(1)
+        load_k(1, slice(0, D))
+        load_q(1, slice(0, D))
+        nc.sync.dma_start(out=gamma_bc[:], in_=ln_gamma.partition_broadcast(P))
+        nc.sync.dma_start(out=beta_bc[:], in_=ln_beta.partition_broadcast(P))
 
         ident_bf = keep.tile([P, P], BF16)
         make_identity(nc, ident_bf[:])
         ident_f32 = keep.tile([P, P], F32)
         make_identity(nc, ident_f32[:])
         neg_half = keep.tile([P, 1], F32)
-        nc.vector.memset(neg_half[:], -0.5)
-        neg_one = keep.tile([P, 2], F32)
-        nc.vector.memset(neg_one[:], -1.0)
-
-        w_scales = keep.tile([P, K_PASSES, D], U8, align_bytes=64)
-        nc.vector.memset(w_scales[:].rearrange("p g n -> p (g n)").bitcast(I32), 0)
-        for quad in range(4):
-            nc.sync.dma_start(
-                out=w_scales[32 * quad : 32 * quad + 4, :, :].bitcast(I32),
-                in_=Wv_scales[:, 4 * quad : 4 * quad + 4, :].rearrange("g r n -> r g n").bitcast(I32),
-            )
-
-        def load_tokens(name, src, b, order):
-            t = keep.tile([P, TILES, D], BF16, name=name + str(b))
-            if order == "words":
-                nc.sync.dma_start(
-                    out=t[:].rearrange("p (u e) d -> p u e d", u=2),
-                    in_=src[b].rearrange("(u p e) d -> p u e d", u=2, e=2),
-                )
-            elif order == "tiles":
-                nc.sync.dma_start(out=t[:], in_=src[b].rearrange("(j p) d -> p j d", j=TILES))
-            else:
-                nc.sync.dma_start(out=t[:], in_=src[b].rearrange("(p j) d -> p j d", j=TILES))
-            return t
-
+        nc.gpsimd.memset(neg_half[:], -0.5)
         ones = keep.tile([P, P], BF16)
         nc.vector.memset(ones[:], 1.0)
-        bv_row = keep.tile([P, D], BF16)
-        nc.vector.memset(bv_row[:], 0.0)
-        nc.sync.dma_start(out=bv_row[0:1, :], in_=bv.rearrange("(o n) -> o n", o=1))
-
-        w_codes = keep.tile([P, K_PASSES, D], U32, align_bytes=64)
-        keys_sb = [load_tokens("keys_sb", keys, 0, "words")]
-        for g in range(K_PASSES):
-            nc.sync.dma_start(
-                out=w_codes[:, g, :].bitcast(I32),
-                in_=Wv_words[g].rearrange("p n t -> p (n t)").bitcast(I32),
-            )
-        k_sb = [load_tokens("k_sb", k_relu, 0, "tiles")]
-        q_sb = [load_tokens("q_sb", q_relu, 0, "rows")]
-        keys_sb.append(load_tokens("keys_sb", keys, 1, "words"))
-        k_sb.append(load_tokens("k_sb", k_relu, 1, "tiles"))
-        q_sb.append(load_tokens("q_sb", q_relu, 1, "rows"))
-        x_sb = [load_tokens("x_sb", queries, bb, "rows") for bb in range(B)]
-        gamma_bc = keep.tile([P, D], BF16)
-        nc.sync.dma_start(out=gamma_bc[:], in_=ln_gamma.partition_broadcast(P))
-        beta_bc = keep.tile([P, D], BF16)
-        nc.sync.dma_start(out=beta_bc[:], in_=ln_beta.partition_broadcast(P))
+        warm = keep.tile([P, 1], F32)
+        nc.vector.memset(warm[:], 0.0)
+        warm_out = keep.tile([P, 1], F32)
+        nc.scalar.activation(out=warm_out[:], in_=warm[:], func=ACT.Exp)
 
         qT = keep.tile([P, B, H, TILES, P], BF16)
         kT = keep.tile([P, B, H, TILES, P], BF16)
@@ -101,45 +124,58 @@ def tile_multiheadattentionlayer_pa_kernel(
         v_scales = keep.tile([P, B, D], U8, align_bytes=64)
         abs_sum = keep.tile([P, TILES, B], F32)
         mask01 = keep.tile([P, TILES, B], F32)
+        bv_bc = keep.tile([P, D], BF16)
+        banks, groupeds = {}, {}
 
-        def transpose_heads(banks, src, dst, b, h0):
-            headsT = banks.tile([P, 2, TILES, P], BF16, tag="prep")
+        def tensor_heads(item):
+            kind, b, h0 = item
+            source = k_sb[b] if kind == "k" else q_sb[b]
+            banks[item] = psum_p.tile([P, 2, TILES, P], BF16, tag="prep", name="headsT")
             for i in range(2):
                 for j in range(TILES):
                     nc.tensor.transpose(
-                        headsT[:, i, j, :], src[:, j, (h0 + i) * DH : (h0 + i + 1) * DH], ident_bf[:]
+                        banks[item][:, i, j, :], source[:, j, (h0 + i) * DH : (h0 + i + 1) * DH], ident_bf[:]
                     )
-            nc.scalar.copy(out=dst[:, b, h0 : h0 + 2, :, :], in_=headsT[:])
 
-        def transpose_keys(banks, b, j):
+        def empty_heads(item):
+            kind, b, h0 = item
+            target = kT if kind == "k" else qT
+            nc.scalar.copy(out=target[:, b, h0 : h0 + 2, :, :], in_=banks[item][:])
+
+        def tensor_keys(item):
+            kind, b, j = item
             keys_words = keys_sb[b][:, j, :].bitcast(F32)
-            keysT = banks.tile([P, K_PASSES, 2, P], F32, tag="prep")
+            banks[item] = psum_p.tile([P, K_PASSES, 2, P], F32, tag="prep", name="keysT")
             for g in range(K_PASSES):
                 for u in range(2):
                     nc.tensor.transpose(
-                        keysT[:, g, u, :], keys_words[:, 256 * g + u : 256 * (g + 1) : 2], ident_f32[:]
+                        banks[item][:, g, u, :], keys_words[:, 256 * g + u : 256 * (g + 1) : 2], ident_f32[:]
                     )
-            nc.vector.tensor_copy(
+
+        def empty_keys(item):
+            kind, b, j = item
+            copy = nc.vector.tensor_copy if b == 0 else nc.scalar.copy
+            copy(
                 out=keys_grouped[b][:].bitcast(F32)[:, :, j * P : (j + 1) * P, :],
-                in_=keysT[:].rearrange("p g u q -> p g q u"),
+                in_=banks[item][:].rearrange("p g u q -> p g q u"),
             )
 
-        def quantise_keys(b):
-            for g in range(K_PASSES):
-                nc.vector.quantize_mx(
-                    out=keys_codes[:, g, b, :].bitcast(FP8X4),
-                    scales=keys_scales[:, g, b, :],
-                    in_=keys_grouped[b][:, g, :, :].rearrange("p q t -> p (q t)"),
-                )
+        def quantise_keys(b, g):
+            nc.vector.quantize_mx(
+                out=keys_codes[:, g, b, :].bitcast(FP8X4),
+                scales=keys_scales[:, g, b, :],
+                in_=keys_grouped[b][:, g, :, :].rearrange("p q t -> p (q t)"),
+            )
 
-        def project_values(banks, b, h):
+        def tensor_values(item):
+            kind, b, h = item
             cols = slice(h * DH, (h + 1) * DH)
-            v_ps = banks.tile([P, TILES, DH], F32, tag="prep")
+            banks[item] = psum_p.tile([P, TILES, DH], F32, tag="prep", name="v_ps")
             for j in range(TILES):
                 toks = slice(j * P, (j + 1) * P)
                 for g in range(K_PASSES):
                     nc.tensor.matmul_mx(
-                        out=v_ps[:, j, :],
+                        out=banks[item][:, j, :],
                         lhsT=keys_codes[:, g, b, toks].bitcast(FP8X4),
                         lhsT_scale=keys_scales[:, g, b, toks],
                         rhs=w_codes[:, g, cols].bitcast(FP8X4),
@@ -147,62 +183,68 @@ def tile_multiheadattentionlayer_pa_kernel(
                         start=(g == 0),
                         stop=(g == K_PASSES - 1),
                     )
-            v_grouped = stage.tile([P, DH, PACK], BF16, align_bytes=64)
+
+        def add_bias(item):
+            kind, b, h = item
+            groupeds[item] = stage.tile([P, DH, PACK], BF16, align_bytes=64, name="v_grouped")
             nc.vector.tensor_tensor(
-                out=v_grouped[:],
-                in0=v_ps[:].rearrange("p j c -> p c j"),
-                in1=bv_bc[:, cols].unsqueeze(2).to_broadcast([P, DH, PACK]),
+                out=groupeds[item][:],
+                in0=banks[item][:].rearrange("p j c -> p c j"),
+                in1=bv_bc[:, h * DH : (h + 1) * DH].unsqueeze(2).to_broadcast([P, DH, PACK]),
                 op=ALU.add,
             )
-            v_flat = v_grouped[:].rearrange("p c j -> p (c j)")
-            nc.vector.tensor_scalar_max(v_flat, v_flat, 0.0)
-            nc.vector.quantize_mx(out=v_codes[:, b, cols].bitcast(FP8X4), scales=v_scales[:, b, cols], in_=v_flat)
 
-        def row_mask(j):
-            for bb in range(B):
-                abs_x = stage.tile([P, D], BF16)
-                nc.scalar.activation(
-                    out=abs_x[:], in_=x_sb[bb][:, j, :], func=ACT.Abs, accum_out=abs_sum[:, j, bb : bb + 1]
-                )
-            nc.vector.tensor_single_scalar(mask01[:, j, :], abs_sum[:, j, :], 0.0, op=ALU.is_gt)
+        def relu(item):
+            v_flat = groupeds[item][:].rearrange("p c j -> p (c j)")
+            nc.gpsimd.tensor_scalar(
+                out=v_flat, in0=v_flat, scalar1=BF16_MAX, scalar2=0.0, op0=ALU.min, op1=ALU.max
+            )
 
-        with tc.psum_pool(name="psum_start", bufs=8) as banks:
-            bv_bc = keep.tile([P, D], BF16)
-            for c in range(D // S):
-                cols = slice(c * S, (c + 1) * S)
-                bv_ps = banks.tile([P, S], F32, tag="prep")
-                nc.tensor.matmul(bv_ps[:], lhsT=ones[:], rhs=bv_row[:, cols], start=True, stop=True)
-                nc.scalar.copy(out=bv_bc[:, cols], in_=bv_ps[:])
-            for b in range(B):
-                for j in range(TILES):
-                    transpose_keys(banks, b, j)
-                quantise_keys(b)
-                for h0 in range(0, H, 2):
-                    transpose_heads(banks, k_sb[b], kT, b, h0)
-                    transpose_heads(banks, q_sb[b], qT, b, h0)
-                    project_values(banks, b, h0)
-                    project_values(banks, b, h0 + 1)
-            for j in range(TILES):
-                row_mask(j)
+        def quantise_values(item):
+            kind, b, h = item
+            cols = slice(h * DH, (h + 1) * DH)
+            nc.vector.quantize_mx(
+                out=v_codes[:, b, cols].bitcast(FP8X4),
+                scales=v_scales[:, b, cols],
+                in_=groupeds[item][:].rearrange("p c j -> p (c j)"),
+            )
 
-        psum_s = ctx.enter_context(tc.psum_pool(name="psum_s", bufs=4))
-        psum_t = ctx.enter_context(tc.psum_pool(name="psum_t", bufs=2))
-        psum_o = ctx.enter_context(tc.psum_pool(name="psum_o", bufs=2))
+        tensor_part = {"k": tensor_heads, "q": tensor_heads, "x": tensor_keys, "v": tensor_values}
 
-        units = [(b, j, h) for b in range(B) for j in range(TILES) for h in range(H)]
-        n_pairs = len(units) // 2
-        n_tiles = n_pairs // 4
-        HALF = D // 2
+        def mask_on_vector(j, bb):
+            nonzero = stage.tile([P, D], BF16, name="nonzero")
+            nc.vector.tensor_scalar(
+                out=nonzero[:],
+                in0=x_sb[bb][:, j, :],
+                scalar1=0.0,
+                scalar2=None,
+                op0=ALU.not_equal,
+                op1=ALU.max,
+                accum_out=mask01[:, j, bb : bb + 1],
+            )
+
+        def mask_on_scalar(j, bb):
+            abs_x = stage.tile([P, D], BF16, name="abs_x")
+            nc.scalar.activation(
+                out=abs_x[:], in_=x_sb[bb][:, j, :], func=ACT.Abs, accum_out=abs_sum[:, j, bb : bb + 1]
+            )
+            nc.vector.tensor_single_scalar(mask01[:, j, bb : bb + 1], abs_sum[:, j, bb : bb + 1], 0.0, op=ALU.is_gt)
+
+        pairs = []
+        for b, js in ((0, (0, 1, 2, 3)), (1, (0, 1)), (1, (2,)), (1, (3,))):
+            pairs += [(b, j, h0) for h0 in range(0, H, 2) for j in js]
+        n_pairs = len(pairs)
+        QUARTER = D // 4
         scores, rowmaxs, shifts, rowsums, es, eTs, e_groupeds, quantised, outputs = {}, {}, {}, {}, {}, {}, {}, {}, {}
-        recips, gains, ys, sums, neg_means, rstds, normeds = {}, {}, {}, {}, {}, {}, {}
+        recips, gains, ys, stats, means, offsets, rstds, normeds = {}, {}, {}, {}, {}, {}, {}, {}
 
-        def score(u):
-            b, j, h = units[u]
-            scores[u] = psum_s.tile([P, S], F32, name="s_ps")
+        def score(pair, i):
+            b, j, h0 = pairs[pair]
+            scores[pair, i] = psum_s.tile([P, S], F32, name="s_ps")
             nc.tensor.matmul(
-                scores[u][:],
-                lhsT=qT[:, b, h, j, :],
-                rhs=kT[:, b, h, :, :].rearrange("p t k -> p (t k)"),
+                scores[pair, i][:],
+                lhsT=qT[:, b, h0 + i, j, :],
+                rhs=kT[:, b, h0 + i, :, :].rearrange("p t k -> p (t k)"),
                 start=True,
                 stop=True,
             )
@@ -210,13 +252,11 @@ def tile_multiheadattentionlayer_pa_kernel(
         def row_max(pair, i):
             if i == 0:
                 rowmaxs[pair] = small.tile([P, 2], F32, name="rowmax")
-            nc.vector.tensor_reduce(
-                out=rowmaxs[pair][:, i : i + 1], in_=scores[2 * pair + i][:], axis=AXIS_X, op=ALU.max
-            )
+            nc.vector.tensor_reduce(out=rowmaxs[pair][:, i : i + 1], in_=scores[pair, i][:], axis=AXIS_X, op=ALU.max)
 
         def shift_of(pair):
             shifts[pair] = small.tile([P, 2], F32, name="shift")
-            nc.vector.tensor_scalar_mul(shifts[pair][:], rowmaxs[pair][:], -SCORE_SCALE)
+            nc.scalar.mul(shifts[pair][:], rowmaxs[pair][:], -SCORE_SCALE)
 
         def exponentiate(pair, i):
             if i == 0:
@@ -224,7 +264,7 @@ def tile_multiheadattentionlayer_pa_kernel(
                 rowsums[pair] = small.tile([P, 2], F32, name="rowsum")
             nc.scalar.activation(
                 out=es[pair][:, i, :],
-                in_=scores[2 * pair + i][:],
+                in_=scores[pair, i][:],
                 func=ACT.Exp,
                 bias=shifts[pair][:, i : i + 1],
                 scale=SCORE_SCALE,
@@ -243,8 +283,8 @@ def tile_multiheadattentionlayer_pa_kernel(
             nc.scalar.copy(out=e_groupeds[pair][:].bitcast(F32), in_=eTs[pair][:].rearrange("p i u q -> p i q u"))
 
         def quantise(pair):
-            e_codes = work.tile([P, 2 * P], U32, align_bytes=64)
-            e_scales = work.tile([P, 2 * P], U8, align_bytes=64)
+            e_codes = work.tile([P, 2 * P], U32, align_bytes=64, name="e_codes")
+            e_scales = work.tile([P, 2 * P], U8, align_bytes=64, name="e_scales")
             nc.vector.quantize_mx(
                 out=e_codes[:].bitcast(FP8X4),
                 scales=e_scales[:],
@@ -253,7 +293,7 @@ def tile_multiheadattentionlayer_pa_kernel(
             quantised[pair] = (e_codes, e_scales)
 
         def multiply(pair):
-            b, j, h0 = units[2 * pair]
+            b, j, h0 = pairs[pair]
             e_codes, e_scales = quantised[pair]
             outputs[pair] = psum_o.tile([P, 2, DH], F32, name="o_ps")
             for i in range(2):
@@ -270,20 +310,20 @@ def tile_multiheadattentionlayer_pa_kernel(
 
         def reciprocal_of(pair):
             recips[pair] = small.tile([P, 2], F32, name="recip")
-            nc.gpsimd.tensor_tensor(out=recips[pair][:], in0=rowsums[pair][:], in1=neg_one[:], op=ALU.pow)
+            nc.vector.reciprocal(out=recips[pair][:], in_=rowsums[pair][:])
 
         def gain_of(pair):
-            j = units[2 * pair][1]
+            j = pairs[pair][1]
             gains[pair] = small.tile([P, 2], F32, name="gain")
             nc.gpsimd.tensor_tensor(out=gains[pair][:], in0=recips[pair][:], in1=mask01[:, j, :], op=ALU.mult)
 
         def residual(pair, i):
-            b, j, h0 = units[2 * pair]
+            b, j, h0 = pairs[pair]
             if h0 == 0 and i == 0:
-                ys[pair // 4] = work.tile([P, D], F32, name="y")
+                ys[b, j] = rows.tile([P, D], F32, name="y")
             cols = slice((h0 + i) * DH, (h0 + i + 1) * DH)
             nc.vector.scalar_tensor_tensor(
-                out=ys[pair // 4][:, cols],
+                out=ys[b, j][:, cols],
                 in0=outputs[pair][:, i, :],
                 scalar=gains[pair][:, i : i + 1],
                 in1=x_sb[b][:, j, cols],
@@ -291,121 +331,197 @@ def tile_multiheadattentionlayer_pa_kernel(
                 op1=ALU.add,
             )
 
-        def sum_y(tile_no, half):
-            if half == 0:
-                sums[tile_no] = small.tile([P, 4], F32, name="sums")
-            unused = stage.tile([P, HALF], BF16, name="unused")
-            nc.scalar.activation(
-                out=unused[:],
-                in_=ys[tile_no][:, half * HALF : (half + 1) * HALF],
-                func=ACT.Identity,
-                accum_out=sums[tile_no][:, half : half + 1],
+        def statistics(t, quarter):
+            if quarter == 0:
+                stats[t] = small.tile([P, 4, 6], F32, name="stats")
+            nc.vector.bn_stats(out=stats[t][:, quarter, :], in_=ys[t][:, quarter * QUARTER : (quarter + 1) * QUARTER])
+
+        def aggregate(t):
+            means[t] = small.tile([P, 2], F32, name="mean_var")
+            nc.vector.bn_aggr(out=means[t][:], in_=stats[t][:].rearrange("p h s -> p (h s)"))
+
+        def rstd_of(t):
+            var_eps = small.tile([P, 1], F32, name="var_eps")
+            nc.gpsimd.tensor_single_scalar(var_eps[:], means[t][:, 1:2], LN_EPS, op=ALU.add)
+            rstds[t] = small.tile([P, 1], F32, name="rstd")
+            nc.gpsimd.tensor_tensor(out=rstds[t][:], in0=var_eps[:], in1=neg_half[:], op=ALU.pow)
+            offsets[t] = small.tile([P, 1], F32, name="offset")
+            nc.gpsimd.tensor_scalar(
+                out=offsets[t][:], in0=means[t][:, 0:1], scalar1=rstds[t][:], scalar2=-1.0, op0=ALU.mult, op1=ALU.mult
+            )
+            normeds[t] = rows.tile([P, D], F32, name="normed")
+
+        def store(t, half):
+            b, j = t
+            cols = slice(half * HALF, (half + 1) * HALF)
+            nc.sync.dma_start(
+                out=out[b].rearrange("(p j) d -> p j d", j=TILES)[:, j, cols], in_=normeds[t][:, cols]
             )
 
-        def mean_of(tile_no):
-            unused = small.tile([P, 2], F32, name="unused2")
-            neg_means[tile_no] = small.tile([P, 1], F32, name="neg_mean")
+        def normalise(t, half):
+            cols = slice(half * HALF, (half + 1) * HALF)
             nc.scalar.activation(
-                out=unused[:], in_=sums[tile_no][:, 0:2], func=ACT.Identity, scale=-1.0 / D, accum_out=neg_means[tile_no][:]
+                out=normeds[t][:, cols], in_=ys[t][:, cols], func=ACT.Identity, scale=rstds[t][:], bias=offsets[t][:]
             )
 
-        def sum_squares(tile_no, half):
-            unused = stage.tile([P, HALF], BF16, name="unused")
-            nc.scalar.activation(
-                out=unused[:],
-                in_=ys[tile_no][:, half * HALF : (half + 1) * HALF],
-                func=ACT.Square,
-                bias=neg_means[tile_no][:],
-                accum_out=sums[tile_no][:, 2 + half : 3 + half],
+        def times_gamma(t, quarter):
+            cols = slice(quarter * QUARTER, (quarter + 1) * QUARTER)
+            nc.gpsimd.tensor_tensor(
+                out=normeds[t][:, cols], in0=normeds[t][:, cols], in1=gamma_bc[:, cols], op=ALU.mult
             )
 
-        def rstd_of(tile_no):
-            unused = small.tile([P, 2], F32, name="unused2")
-            var_eps = small.tile([P, 1], F32)
-            nc.scalar.activation(
-                out=unused[:], in_=sums[tile_no][:, 2:4], func=ACT.Identity, scale=1.0 / D, bias=LN_EPS / 2, accum_out=var_eps[:]
+        def plus_beta(t, quarter):
+            cols = slice(quarter * QUARTER, (quarter + 1) * QUARTER)
+            nc.gpsimd.tensor_tensor(
+                out=normeds[t][:, cols], in0=normeds[t][:, cols], in1=beta_bc[:, cols], op=ALU.add
             )
-            rstds[tile_no] = small.tile([P, 1], F32, name="rstd")
-            nc.gpsimd.tensor_tensor(out=rstds[tile_no][:], in0=var_eps[:], in1=neg_half[:], op=ALU.pow)
+            if quarter % 2 == 1:
+                store(t, quarter // 2)
 
-        def centre(tile_no, half):
-            if half == 0:
-                normeds[tile_no] = work.tile([P, D], F32, name="normed")
+        def centre(t, half):
             cols = slice(half * HALF, (half + 1) * HALF)
             nc.vector.scalar_tensor_tensor(
-                out=normeds[tile_no][:, cols],
-                in0=ys[tile_no][:, cols],
-                scalar=neg_means[tile_no][:],
+                out=normeds[t][:, cols],
+                in0=ys[t][:, cols],
+                scalar=means[t][:, 0:1],
                 in1=gamma_bc[:, cols],
-                op0=ALU.add,
+                op0=ALU.subtract,
                 op1=ALU.mult,
             )
 
-        def scale_and_store(tile_no, half):
-            b, j = tile_no // TILES, tile_no % TILES
+        def scale_and_store(t, half):
             cols = slice(half * HALF, (half + 1) * HALF)
             nc.vector.scalar_tensor_tensor(
-                out=normeds[tile_no][:, cols],
-                in0=normeds[tile_no][:, cols],
-                scalar=rstds[tile_no][:],
+                out=normeds[t][:, cols],
+                in0=normeds[t][:, cols],
+                scalar=rstds[t][:],
                 in1=beta_bc[:, cols],
                 op0=ALU.mult,
                 op1=ALU.add,
             )
-            nc.sync.dma_start(
-                out=out[b].rearrange("(p j) d -> p j d", j=TILES)[:, j, cols], in_=normeds[tile_no][:, cols]
+            store(t, half)
+
+        for kind in ("k", "q"):
+            tensor_heads((kind, 0, 0))
+            empty_heads((kind, 0, 0))
+        for c in range(2):
+            bv_ps = psum_p.tile([P, HALF], F32, tag="prep", name="bv_ps")
+            nc.tensor.matmul(
+                bv_ps[:], lhsT=ones[:], rhs=bv_row[:, c * HALF : (c + 1) * HALF], start=True, stop=True
             )
+            nc.scalar.copy(out=bv_bc[:, c * HALF : (c + 1) * HALF], in_=bv_ps[:])
+        for pair in range(2):
+            for i in range(2):
+                score(pair, i)
+        for pair in range(2):
+            for i in range(2):
+                row_max(pair, i)
+        for kind in ("k", "q"):
+            tensor_heads((kind, 0, 2))
+            empty_heads((kind, 0, 2))
+        for j in range(TILES):
+            tensor_keys(("x", 0, j))
+            empty_keys(("x", 0, j))
+        for g in range(K_PASSES):
+            quantise_keys(0, g)
+        shift_of(0)
 
-        with tc.manual_schedule():
-            for u in range(4):
-                score(u)
-            row_max(0, 0)
-            row_max(0, 1)
-            shift_of(0)
-            for s in range(n_pairs + 10):
-                stats_tile, stats_piece = divmod(s - 6, 4)
-                apply_tile, apply_piece = divmod(s - 9, 4)
-                multiplying = 0 <= s - 2 < n_pairs
-                finishing = 0 <= s - 3 < n_pairs
-                ahead = s + 1 < n_pairs
+        scalar_prep = [(kind, 0, h0) for h0 in (4, 6) for kind in ("k", "q")]
+        scalar_prep += [("x", 1, j) for j in range(TILES)]
+        scalar_prep += [(kind, 1, h0) for h0 in range(0, H, 2) for kind in ("k", "q")]
+        vector_prep = [("v", b, h) for b in range(B) for h in range(H)]
 
-                if multiplying:
-                    reciprocal_of(s - 2)
-                    gain_of(s - 2)
-                    quantise(s - 2)
-                if ahead:
-                    row_max(s + 1, 0)
-                    row_max(s + 1, 1)
-                if finishing:
-                    residual(s - 3, 0)
-                if ahead:
-                    shift_of(s + 1)
-                if finishing:
-                    residual(s - 3, 1)
+        VECTOR_TILES = ((B - 1, TILES - 2), (B - 1, TILES - 1))
+        vector_ln, scalar_ln, gpsimd_ln = [], [], []
+        filled, biased, complete = [], [], []
+        for s in range(n_pairs + 12):
+            ahead = 0 < s and s + 1 < n_pairs
+            dividing = 0 <= s - 2 < n_pairs
+            finishing = 0 <= s - 3 < n_pairs
+            if 0 < s < n_pairs:
+                shift_of(s)
+            if s < n_pairs:
+                exponentiate(s, 0)
+            if 0 <= s - 1 < n_pairs:
+                regroup(s - 1)
+            if s < n_pairs:
+                exponentiate(s, 1)
+            for item in filled:
+                if item[0] in ("k", "q"):
+                    empty_heads(item)
+                elif item[0] == "x":
+                    empty_keys(item)
+            if s + 2 < n_pairs:
+                score(s + 2, 0)
+            if s < n_pairs:
+                transpose_e(s, 0)
+            if s < n_pairs:
+                transpose_e(s, 1)
+            if s + 2 < n_pairs:
+                score(s + 2, 1)
+            if ahead:
+                row_max(s + 1, 0)
+            if dividing:
+                quantise(s - 2)
+            for item in biased:
+                quantise_values(item)
+            if 0 <= s - 1 < n_pairs:
+                reciprocal_of(s - 1)
+                gain_of(s - 1)
+            for t in complete:
+                aggregate(t)
+            if finishing:
+                residual(s - 3, 0)
+            if finishing:
+                residual(s - 3, 1)
+            if ahead:
+                row_max(s + 1, 1)
+            biased = [item for item in filled if item[0] == "v"]
+            for item in biased:
+                add_bias(item)
+            for item in biased:
+                relu(item)
+            if s == 10:
+                for g in range(K_PASSES):
+                    quantise_keys(1, g)
+            if dividing:
+                multiply(s - 2)
+            filled = []
+            take = 2 if s == 0 else 1 if s % 2 == 0 or s > 16 else 0
+            filled += vector_prep[:take]
+            vector_prep = vector_prep[take:]
+            take = 1 if s > 0 else 0
+            filled += scalar_prep[:take]
+            scalar_prep = scalar_prep[take:]
+            for item in filled:
+                tensor_part[item[0]](item)
 
-                for i in range(2):
-                    if s < n_pairs:
-                        exponentiate(s, i)
-                        transpose_e(s, i)
-                    if 2 * (s + 2) + i < len(units):
-                        score(2 * (s + 2) + i)
-                    if i == 0:
-                        if multiplying:
-                            multiply(s - 2)
-                        if 0 <= stats_tile < n_tiles and stats_piece == 2:
-                            mean_of(stats_tile)
-                        if 0 <= stats_tile - 1 < n_tiles and stats_piece == 0:
-                            rstd_of(stats_tile - 1)
-                if 0 <= s - 1 < n_pairs:
-                    regroup(s - 1)
-                if 0 <= stats_tile < n_tiles:
-                    if stats_piece < 2:
-                        sum_y(stats_tile, stats_piece)
-                    else:
-                        sum_squares(stats_tile, stats_piece - 2)
-
-                if 0 <= apply_tile < n_tiles:
-                    if apply_piece < 2:
-                        centre(apply_tile, apply_piece)
-                    else:
-                        scale_and_store(apply_tile, apply_piece - 2)
+            if s < 4:
+                mask_on_vector(s, 0)
+                mask_on_scalar(s, 1)
+            for function, t, part in scalar_ln[:1]:
+                function(t, part)
+            scalar_ln = scalar_ln[1:]
+            for function, t, part in gpsimd_ln[:3]:
+                function(t, part)
+            gpsimd_ln = gpsimd_ln[3:]
+            for t in complete:
+                rstd_of(t)
+                if t in VECTOR_TILES:
+                    vector_ln += [(centre, t, half) for half in range(2)]
+                    vector_ln += [(scale_and_store, t, half) for half in range(2)]
+                else:
+                    for half in range(2):
+                        scalar_ln.append((normalise, t, half))
+                        for piece in (times_gamma, plus_beta):
+                            gpsimd_ln += [(piece, t, 2 * half), (piece, t, 2 * half + 1)]
+            for function, t, part in vector_ln[:2]:
+                function(t, part)
+            vector_ln = vector_ln[2:]
+            complete = []
+            if finishing:
+                b, j, h0 = pairs[s - 3]
+                statistics((b, j), h0 // 2)
+                if h0 == H - 2:
+                    complete.append((b, j))
+        assert not (vector_ln or scalar_ln or gpsimd_ln or scalar_prep or vector_prep or filled or biased)

@@ -22,7 +22,6 @@ TILES = S // P
 K_PASSES = D // (P * PACK)
 SCORE_SCALE = 1.0 / math.sqrt(DH)
 LN_EPS = 1e-8
-BF16_MAX = 255.0 * 2.0**120
 
 FLOPS = 2 * B * S * D * D + 2 * (2 * B * H * S * S * DH)
 
@@ -106,6 +105,8 @@ def tile_multiheadattentionlayer_pa_kernel(
         make_identity(nc, ident_f32[:])
         neg_half = keep.tile([P, 1], F32)
         nc.gpsimd.memset(neg_half[:], -0.5)
+        neg_one = keep.tile([P, 2], F32)
+        nc.gpsimd.memset(neg_one[:], -1.0)
         ones = keep.tile([P, P], BF16)
         nc.vector.memset(ones[:], 1.0)
         warm = keep.tile([P, 1], F32)
@@ -196,9 +197,7 @@ def tile_multiheadattentionlayer_pa_kernel(
 
         def relu(item):
             v_flat = groupeds[item][:].rearrange("p c j -> p (c j)")
-            nc.gpsimd.tensor_scalar(
-                out=v_flat, in0=v_flat, scalar1=BF16_MAX, scalar2=0.0, op0=ALU.min, op1=ALU.max
-            )
+            nc.vector.tensor_scalar_max(v_flat, v_flat, 0.0)
 
         def quantise_values(item):
             kind, b, h = item
@@ -236,7 +235,7 @@ def tile_multiheadattentionlayer_pa_kernel(
         n_pairs = len(pairs)
         QUARTER = D // 4
         scores, rowmaxs, shifts, rowsums, es, eTs, e_groupeds, quantised, outputs = {}, {}, {}, {}, {}, {}, {}, {}, {}
-        recips, gains, ys, stats, means, offsets, rstds, normeds = {}, {}, {}, {}, {}, {}, {}, {}
+        recips, gains, ys, stats, means, neg_means, sums, rstds, normeds = {}, {}, {}, {}, {}, {}, {}, {}, {}
 
         def score(pair, i):
             b, j, h0 = pairs[pair]
@@ -310,7 +309,7 @@ def tile_multiheadattentionlayer_pa_kernel(
 
         def reciprocal_of(pair):
             recips[pair] = small.tile([P, 2], F32, name="recip")
-            nc.vector.reciprocal(out=recips[pair][:], in_=rowsums[pair][:])
+            nc.gpsimd.tensor_tensor(out=recips[pair][:], in0=rowsums[pair][:], in1=neg_one[:], op=ALU.pow)
 
         def gain_of(pair):
             j = pairs[pair][1]
@@ -331,6 +330,43 @@ def tile_multiheadattentionlayer_pa_kernel(
                 op1=ALU.add,
             )
 
+        def sum_y(t, half):
+            if half == 0:
+                sums[t] = small.tile([P, 4], F32, name="sums")
+            unused = stage.tile([P, HALF], BF16, name="unused")
+            nc.scalar.activation(
+                out=unused[:],
+                in_=ys[t][:, half * HALF : (half + 1) * HALF],
+                func=ACT.Identity,
+                accum_out=sums[t][:, half : half + 1],
+            )
+
+        def mean_of(t, part):
+            unused = small.tile([P, 2], F32, name="unused2")
+            neg_means[t] = small.tile([P, 1], F32, name="neg_mean")
+            nc.scalar.activation(
+                out=unused[:], in_=sums[t][:, 0:2], func=ACT.Identity, scale=-1.0 / D, accum_out=neg_means[t][:]
+            )
+
+        def sum_squares(t, half):
+            unused = stage.tile([P, HALF], BF16, name="unused")
+            nc.scalar.activation(
+                out=unused[:],
+                in_=ys[t][:, half * HALF : (half + 1) * HALF],
+                func=ACT.Square,
+                bias=neg_means[t][:],
+                accum_out=sums[t][:, 2 + half : 3 + half],
+            )
+
+        def rstd_from_squares(t, part):
+            unused = small.tile([P, 2], F32, name="unused2")
+            var_eps = small.tile([P, 1], F32, name="var_eps")
+            nc.scalar.activation(
+                out=unused[:], in_=sums[t][:, 2:4], func=ACT.Identity, scale=1.0 / D, bias=LN_EPS / 2, accum_out=var_eps[:]
+            )
+            rstds[t] = small.tile([P, 1], F32, name="rstd")
+            nc.gpsimd.tensor_tensor(out=rstds[t][:], in0=var_eps[:], in1=neg_half[:], op=ALU.pow)
+
         def statistics(t, quarter):
             if quarter == 0:
                 stats[t] = small.tile([P, 4, 6], F32, name="stats")
@@ -345,11 +381,8 @@ def tile_multiheadattentionlayer_pa_kernel(
             nc.gpsimd.tensor_single_scalar(var_eps[:], means[t][:, 1:2], LN_EPS, op=ALU.add)
             rstds[t] = small.tile([P, 1], F32, name="rstd")
             nc.gpsimd.tensor_tensor(out=rstds[t][:], in0=var_eps[:], in1=neg_half[:], op=ALU.pow)
-            offsets[t] = small.tile([P, 1], F32, name="offset")
-            nc.gpsimd.tensor_scalar(
-                out=offsets[t][:], in0=means[t][:, 0:1], scalar1=rstds[t][:], scalar2=-1.0, op0=ALU.mult, op1=ALU.mult
-            )
-            normeds[t] = rows.tile([P, D], F32, name="normed")
+            neg_means[t] = small.tile([P, 1], F32, name="neg_mean")
+            nc.vector.tensor_scalar_mul(neg_means[t][:], means[t][:, 0:1], -1.0)
 
         def store(t, half):
             b, j = t
@@ -358,34 +391,16 @@ def tile_multiheadattentionlayer_pa_kernel(
                 out=out[b].rearrange("(p j) d -> p j d", j=TILES)[:, j, cols], in_=normeds[t][:, cols]
             )
 
-        def normalise(t, half):
-            cols = slice(half * HALF, (half + 1) * HALF)
-            nc.scalar.activation(
-                out=normeds[t][:, cols], in_=ys[t][:, cols], func=ACT.Identity, scale=rstds[t][:], bias=offsets[t][:]
-            )
-
-        def times_gamma(t, quarter):
-            cols = slice(quarter * QUARTER, (quarter + 1) * QUARTER)
-            nc.gpsimd.tensor_tensor(
-                out=normeds[t][:, cols], in0=normeds[t][:, cols], in1=gamma_bc[:, cols], op=ALU.mult
-            )
-
-        def plus_beta(t, quarter):
-            cols = slice(quarter * QUARTER, (quarter + 1) * QUARTER)
-            nc.gpsimd.tensor_tensor(
-                out=normeds[t][:, cols], in0=normeds[t][:, cols], in1=beta_bc[:, cols], op=ALU.add
-            )
-            if quarter % 2 == 1:
-                store(t, quarter // 2)
-
         def centre(t, half):
+            if half == 0:
+                normeds[t] = work.tile([P, D], F32, name="normed")
             cols = slice(half * HALF, (half + 1) * HALF)
             nc.vector.scalar_tensor_tensor(
                 out=normeds[t][:, cols],
                 in0=ys[t][:, cols],
-                scalar=means[t][:, 0:1],
+                scalar=neg_means[t][:],
                 in1=gamma_bc[:, cols],
-                op0=ALU.subtract,
+                op0=ALU.add,
                 op1=ALU.mult,
             )
 
@@ -432,7 +447,7 @@ def tile_multiheadattentionlayer_pa_kernel(
         vector_prep = [("v", b, h) for b in range(B) for h in range(H)]
 
         VECTOR_TILES = ((B - 1, TILES - 2), (B - 1, TILES - 1))
-        vector_ln, scalar_ln, gpsimd_ln = [], [], []
+        vector_ln, scalar_ln = [], []
         filled, biased, complete = [], [], []
         for s in range(n_pairs + 12):
             ahead = 0 < s and s + 1 < n_pairs
@@ -444,6 +459,14 @@ def tile_multiheadattentionlayer_pa_kernel(
                 exponentiate(s, 0)
             if 0 <= s - 1 < n_pairs:
                 regroup(s - 1)
+            take = 2
+            pieces, scalar_ln = scalar_ln[:take], scalar_ln[take:]
+            for function, t, part in pieces:
+                function(t, part)
+                if function is mean_of:
+                    vector_ln += [(centre, t, 0), (centre, t, 1)]
+                elif function is rstd_from_squares:
+                    vector_ln += [(scale_and_store, t, 0), (scale_and_store, t, 1)]
             if s < n_pairs:
                 exponentiate(s, 1)
             for item in filled:
@@ -461,15 +484,16 @@ def tile_multiheadattentionlayer_pa_kernel(
                 score(s + 2, 1)
             if ahead:
                 row_max(s + 1, 0)
+            for item in biased:
+                relu(item)
             if dividing:
                 quantise(s - 2)
             for item in biased:
                 quantise_values(item)
             if 0 <= s - 1 < n_pairs:
                 reciprocal_of(s - 1)
-                gain_of(s - 1)
-            for t in complete:
-                aggregate(t)
+            if dividing:
+                gain_of(s - 2)
             if finishing:
                 residual(s - 3, 0)
             if finishing:
@@ -479,11 +503,13 @@ def tile_multiheadattentionlayer_pa_kernel(
             biased = [item for item in filled if item[0] == "v"]
             for item in biased:
                 add_bias(item)
-            for item in biased:
-                relu(item)
             if s == 10:
                 for g in range(K_PASSES):
                     quantise_keys(1, g)
+            take = 2 if s < n_pairs + 3 else 4
+            for function, t, part in vector_ln[:take]:
+                function(t, part)
+            vector_ln = vector_ln[take:]
             if dividing:
                 multiply(s - 2)
             filled = []
@@ -496,32 +522,21 @@ def tile_multiheadattentionlayer_pa_kernel(
             for item in filled:
                 tensor_part[item[0]](item)
 
-            if s < 4:
-                mask_on_vector(s, 0)
-                mask_on_scalar(s, 1)
-            for function, t, part in scalar_ln[:1]:
-                function(t, part)
-            scalar_ln = scalar_ln[1:]
-            for function, t, part in gpsimd_ln[:3]:
-                function(t, part)
-            gpsimd_ln = gpsimd_ln[3:]
-            for t in complete:
-                rstd_of(t)
-                if t in VECTOR_TILES:
-                    vector_ln += [(centre, t, half) for half in range(2)]
-                    vector_ln += [(scale_and_store, t, half) for half in range(2)]
-                else:
-                    for half in range(2):
-                        scalar_ln.append((normalise, t, half))
-                        for piece in (times_gamma, plus_beta):
-                            gpsimd_ln += [(piece, t, 2 * half), (piece, t, 2 * half + 1)]
-            for function, t, part in vector_ln[:2]:
-                function(t, part)
-            vector_ln = vector_ln[2:]
-            complete = []
+            if 1 <= s < 5:
+                mask_on_vector(s - 1, 0)
+                mask_on_scalar(s - 1, 1)
             if finishing:
-                b, j, h0 = pairs[s - 3]
-                statistics((b, j), h0 // 2)
-                if h0 == H - 2:
-                    complete.append((b, j))
-        assert not (vector_ln or scalar_ln or gpsimd_ln or scalar_prep or vector_prep or filled or biased)
+                t, h0 = pairs[s - 3][:2], pairs[s - 3][2]
+                if t in VECTOR_TILES:
+                    statistics(t, h0 // 2)
+                    if h0 == H - 2:
+                        aggregate(t)
+                        rstd_of(t)
+                        vector_ln += [(centre, t, 0), (centre, t, 1)]
+                        vector_ln += [(scale_and_store, t, 0), (scale_and_store, t, 1)]
+                elif h0 == 2:
+                    scalar_ln.append((sum_y, t, 0))
+                elif h0 == H - 2:
+                    scalar_ln += [(sum_y, t, 1), (mean_of, t, None), (sum_squares, t, 0), (sum_squares, t, 1)]
+                    scalar_ln.append((rstd_from_squares, t, None))
+        assert not (vector_ln or scalar_ln or scalar_prep or vector_prep or filled or biased)

@@ -72,17 +72,15 @@ def tile_multiheadattentionlayer_pa_kernel(
         nc.vector.memset(bv_row[:], 0.0)
         nc.vector.memset(w_scales[:].rearrange("p g n -> p (g n)").bitcast(I32), 0)
 
-        load_k(0, slice(0, HALF // 2))
-        load_q(0, slice(0, HALF // 2))
-        nc.sync.dma_start(out=bv_row[0:1, :], in_=bv.rearrange("(o n) -> o n", o=1))
-        load_k(0, slice(HALF // 2, HALF))
-        load_q(0, slice(HALF // 2, HALF))
-        load_keys(0)
         for quad in range(4):
             nc.sync.dma_start(
                 out=w_scales[32 * quad : 32 * quad + 4, :, :].bitcast(I32),
                 in_=Wv_scales[:, 4 * quad : 4 * quad + 4, :].rearrange("g r n -> r g n").bitcast(I32),
             )
+        load_k(0, slice(0, HALF))
+        load_q(0, slice(0, HALF))
+        nc.sync.dma_start(out=bv_row[0:1, :], in_=bv.rearrange("(o n) -> o n", o=1))
+        load_keys(0)
         for g in range(K_PASSES):
             nc.sync.dma_start(
                 out=w_codes[:, g, :].bitcast(I32),
@@ -441,8 +439,9 @@ def tile_multiheadattentionlayer_pa_kernel(
             quantise_keys(0, g)
         shift_of(0)
 
-        scalar_prep = [(kind, 0, h0) for h0 in (4, 6) for kind in ("k", "q")]
+        scalar_prep = [(kind, 0, 4) for kind in ("k", "q")]
         scalar_prep += [("x", 1, j) for j in range(TILES)]
+        scalar_prep += [(kind, 0, 6) for kind in ("k", "q")]
         scalar_prep += [(kind, 1, h0) for h0 in range(0, H, 2) for kind in ("k", "q")]
         vector_prep = [("v", b, h) for b in range(B) for h in range(H)]
 
@@ -453,27 +452,12 @@ def tile_multiheadattentionlayer_pa_kernel(
             ahead = 0 < s and s + 1 < n_pairs
             dividing = 0 <= s - 2 < n_pairs
             finishing = 0 <= s - 3 < n_pairs
-            if 0 < s < n_pairs:
-                shift_of(s)
             if s < n_pairs:
                 exponentiate(s, 0)
             if 0 <= s - 1 < n_pairs:
                 regroup(s - 1)
-            take = 2
-            pieces, scalar_ln = scalar_ln[:take], scalar_ln[take:]
-            for function, t, part in pieces:
-                function(t, part)
-                if function is mean_of:
-                    vector_ln += [(centre, t, 0), (centre, t, 1)]
-                elif function is rstd_from_squares:
-                    vector_ln += [(scale_and_store, t, 0), (scale_and_store, t, 1)]
             if s < n_pairs:
                 exponentiate(s, 1)
-            for item in filled:
-                if item[0] in ("k", "q"):
-                    empty_heads(item)
-                elif item[0] == "x":
-                    empty_keys(item)
             if s + 2 < n_pairs:
                 score(s + 2, 0)
             if s < n_pairs:
@@ -484,6 +468,12 @@ def tile_multiheadattentionlayer_pa_kernel(
                 score(s + 2, 1)
             if ahead:
                 row_max(s + 1, 0)
+            if ahead:
+                row_max(s + 1, 1)
+            if finishing:
+                residual(s - 3, 0)
+            if finishing:
+                residual(s - 3, 1)
             for item in biased:
                 relu(item)
             if dividing:
@@ -494,26 +484,35 @@ def tile_multiheadattentionlayer_pa_kernel(
                 reciprocal_of(s - 1)
             if dividing:
                 gain_of(s - 2)
-            if finishing:
-                residual(s - 3, 0)
-            if finishing:
-                residual(s - 3, 1)
-            if ahead:
-                row_max(s + 1, 1)
             biased = [item for item in filled if item[0] == "v"]
             for item in biased:
                 add_bias(item)
-            if s == 10:
+            if s == 8:
                 for g in range(K_PASSES):
                     quantise_keys(1, g)
             take = 2 if s < n_pairs + 3 else 4
             for function, t, part in vector_ln[:take]:
                 function(t, part)
             vector_ln = vector_ln[take:]
-            if dividing:
+            for item in filled:
+                if item[0] in ("k", "q"):
+                    empty_heads(item)
+                elif item[0] == "x":
+                    empty_keys(item)
+            if s + 1 < n_pairs:
+                shift_of(s + 1)
+            take = 2
+            pieces, scalar_ln = scalar_ln[:take], scalar_ln[take:]
+            for function, t, part in pieces:
+                function(t, part)
+                if function is mean_of:
+                    vector_ln += [(centre, t, 0), (centre, t, 1)]
+                elif function is rstd_from_squares:
+                    vector_ln += [(scale_and_store, t, 0), (scale_and_store, t, 1)]
+            if 0 <= s - 2 < n_pairs:
                 multiply(s - 2)
             filled = []
-            take = 2 if s == 0 else 1 if s % 2 == 0 or s > 16 else 0
+            take = 2 if s == 0 else 0 if s in (7, 8) else 1
             filled += vector_prep[:take]
             vector_prep = vector_prep[take:]
             take = 1 if s > 0 else 0

@@ -72,13 +72,13 @@ def tile_multiheadattentionlayer_pa_kernel(
         nc.vector.memset(bv_row[:], 0.0)
         nc.vector.memset(w_scales[:].rearrange("p g n -> p (g n)").bitcast(I32), 0)
 
+        load_k(0, slice(0, HALF))
+        load_q(0, slice(0, HALF))
         for quad in range(4):
             nc.sync.dma_start(
                 out=w_scales[32 * quad : 32 * quad + 4, :, :].bitcast(I32),
                 in_=Wv_scales[:, 4 * quad : 4 * quad + 4, :].rearrange("g r n -> r g n").bitcast(I32),
             )
-        load_k(0, slice(0, HALF))
-        load_q(0, slice(0, HALF))
         nc.sync.dma_start(out=bv_row[0:1, :], in_=bv.rearrange("(o n) -> o n", o=1))
         load_keys(0)
         for g in range(K_PASSES):
@@ -238,6 +238,16 @@ def tile_multiheadattentionlayer_pa_kernel(
         def score(pair, i):
             b, j, h0 = pairs[pair]
             scores[pair, i] = psum_s.tile([P, S], F32, name="s_ps")
+            if pair >= 2 and i == 0:
+                nc.tensor.matmul_mx(
+                    out=scores[pair, i][:, 0:512],
+                    lhsT=w_codes[:, 0, 0:P].bitcast(FP8X4),
+                    lhsT_scale=w_scales[:, 0, 0:P],
+                    rhs=w_codes[:, 0, 0:512].bitcast(FP8X4),
+                    rhs_scale=w_scales[:, 0, 0:512],
+                    start=True,
+                    stop=True,
+                )
             nc.tensor.matmul(
                 scores[pair, i][:],
                 lhsT=qT[:, b, h0 + i, j, :],
@@ -379,8 +389,6 @@ def tile_multiheadattentionlayer_pa_kernel(
             nc.gpsimd.tensor_single_scalar(var_eps[:], means[t][:, 1:2], LN_EPS, op=ALU.add)
             rstds[t] = small.tile([P, 1], F32, name="rstd")
             nc.gpsimd.tensor_tensor(out=rstds[t][:], in0=var_eps[:], in1=neg_half[:], op=ALU.pow)
-            neg_means[t] = small.tile([P, 1], F32, name="neg_mean")
-            nc.vector.tensor_scalar_mul(neg_means[t][:], means[t][:, 0:1], -1.0)
 
         def store(t, half):
             b, j = t
@@ -393,12 +401,13 @@ def tile_multiheadattentionlayer_pa_kernel(
             if half == 0:
                 normeds[t] = work.tile([P, D], F32, name="normed")
             cols = slice(half * HALF, (half + 1) * HALF)
+            by_vector = t in VECTOR_TILES
             nc.vector.scalar_tensor_tensor(
                 out=normeds[t][:, cols],
                 in0=ys[t][:, cols],
-                scalar=neg_means[t][:],
+                scalar=means[t][:, 0:1] if by_vector else neg_means[t][:],
                 in1=gamma_bc[:, cols],
-                op0=ALU.add,
+                op0=ALU.subtract if by_vector else ALU.add,
                 op1=ALU.mult,
             )
 
@@ -445,7 +454,7 @@ def tile_multiheadattentionlayer_pa_kernel(
         scalar_prep += [(kind, 1, h0) for h0 in range(0, H, 2) for kind in ("k", "q")]
         vector_prep = [("v", b, h) for b in range(B) for h in range(H)]
 
-        VECTOR_TILES = ((B - 1, TILES - 2), (B - 1, TILES - 1))
+        VECTOR_TILES = ((1, 2), (1, 3))
         vector_ln, scalar_ln = [], []
         filled, biased, complete = [], [], []
         for s in range(n_pairs + 12):

@@ -105,6 +105,8 @@ def tile_multiheadattentionlayer_pa_kernel(
         nc.gpsimd.memset(neg_half[:], -0.5)
         neg_one = keep.tile([P, 2], F32)
         nc.gpsimd.memset(neg_one[:], -1.0)
+        zeros = keep.tile([P, HALF], BF16)
+        nc.vector.memset(zeros[:], 0.0)
         ones = keep.tile([P, P], BF16)
         nc.vector.memset(ones[:], 1.0)
         warm = keep.tile([P, 1], F32)
@@ -144,7 +146,11 @@ def tile_multiheadattentionlayer_pa_kernel(
         def tensor_keys(item):
             kind, b, j = item
             keys_words = keys_sb[b][:, j, :].bitcast(F32)
-            banks[item] = psum_p.tile([P, K_PASSES, 2, P], F32, tag="prep", name="keysT")
+            if b == 0 and j >= 2:
+                pool, tag = ((psum_t, "eT"), (psum_o, "o_ps"))[j - 2]
+            else:
+                pool, tag = psum_p, "prep"
+            banks[item] = pool.tile([P, K_PASSES, 2, P], F32, tag=tag, name="keysT")
             for g in range(K_PASSES):
                 for u in range(2):
                     nc.tensor.transpose(
@@ -153,7 +159,7 @@ def tile_multiheadattentionlayer_pa_kernel(
 
         def empty_keys(item):
             kind, b, j = item
-            copy = nc.vector.tensor_copy if b == 0 else nc.scalar.copy
+            copy = nc.vector.tensor_copy if b == 0 and j % 2 == 0 else nc.scalar.copy
             copy(
                 out=keys_grouped[b][:].bitcast(F32)[:, :, j * P : (j + 1) * P, :],
                 in_=banks[item][:].rearrange("p g u q -> p g q u"),
@@ -423,27 +429,35 @@ def tile_multiheadattentionlayer_pa_kernel(
             )
             store(t, half)
 
+        spare = psum_o.tile([P, HALF], F32, name="o_ps")
+
+        def keep_warm():
+            nc.tensor.matmul(spare[:], lhsT=ones[:], rhs=zeros[:], start=True, stop=True)
+
+        for i in range(4):
+            keep_warm()
         for kind in ("k", "q"):
             tensor_heads((kind, 0, 0))
             empty_heads((kind, 0, 0))
+            keep_warm()
         for c in range(2):
             bv_ps = psum_p.tile([P, HALF], F32, tag="prep", name="bv_ps")
             nc.tensor.matmul(
                 bv_ps[:], lhsT=ones[:], rhs=bv_row[:, c * HALF : (c + 1) * HALF], start=True, stop=True
             )
-            nc.scalar.copy(out=bv_bc[:, c * HALF : (c + 1) * HALF], in_=bv_ps[:])
+            nc.vector.tensor_copy(out=bv_bc[:, c * HALF : (c + 1) * HALF], in_=bv_ps[:])
         for pair in range(2):
             for i in range(2):
                 score(pair, i)
         for pair in range(2):
             for i in range(2):
                 row_max(pair, i)
-        for kind in ("k", "q"):
-            tensor_heads((kind, 0, 2))
-            empty_heads((kind, 0, 2))
         for j in range(TILES):
             tensor_keys(("x", 0, j))
             empty_keys(("x", 0, j))
+        first = [(kind, 0, 2) for kind in ("k", "q")]
+        for item in first:
+            tensor_heads(item)
         for g in range(K_PASSES):
             quantise_keys(0, g)
         shift_of(0)
@@ -456,7 +470,7 @@ def tile_multiheadattentionlayer_pa_kernel(
 
         VECTOR_TILES = ((1, 2), (1, 3))
         vector_ln, scalar_ln = [], []
-        filled, biased, complete = [], [], []
+        filled, biased, complete = first, [], []
         for s in range(n_pairs + 12):
             ahead = 0 < s and s + 1 < n_pairs
             dividing = 0 <= s - 2 < n_pairs

@@ -69,8 +69,12 @@ def tile_multiheadattentionlayer_pa_kernel(
                     in_=keys[b].rearrange("(u p e) d -> p u e d", u=2, e=2)[:, u, :, :],
                 )
 
-        nc.vector.memset(bv_row[:], 0.0)
+        ones = keep.tile([P, P], BF16)
+        nc.vector.memset(ones[:], 1.0)
+        zeros = keep.tile([P, HALF], BF16)
+        nc.vector.memset(zeros[:], 0.0)
         nc.vector.memset(w_scales[:].rearrange("p g n -> p (g n)").bitcast(I32), 0)
+        nc.vector.memset(bv_row[:], 0.0)
 
         load_k(0, slice(0, HALF))
         load_q(0, slice(0, HALF))
@@ -103,14 +107,8 @@ def tile_multiheadattentionlayer_pa_kernel(
         make_identity(nc, ident_f32[:])
         neg_half = keep.tile([P, 1], F32)
         nc.gpsimd.memset(neg_half[:], -0.5)
-        neg_one = keep.tile([P, 2], F32)
-        nc.gpsimd.memset(neg_one[:], -1.0)
-        zeros = keep.tile([P, HALF], BF16)
-        nc.vector.memset(zeros[:], 0.0)
-        ones = keep.tile([P, P], BF16)
-        nc.vector.memset(ones[:], 1.0)
         warm = keep.tile([P, 1], F32)
-        nc.vector.memset(warm[:], 0.0)
+        nc.vector.memset(warm[:], 1.0)
         warm_out = keep.tile([P, 1], F32)
         nc.scalar.activation(out=warm_out[:], in_=warm[:], func=ACT.Exp)
 
@@ -323,7 +321,7 @@ def tile_multiheadattentionlayer_pa_kernel(
 
         def reciprocal_of(pair):
             recips[pair] = small.tile([P, 2], F32, name="recip")
-            nc.gpsimd.tensor_tensor(out=recips[pair][:], in0=rowsums[pair][:], in1=neg_one[:], op=ALU.pow)
+            nc.vector.reciprocal(out=recips[pair][:], in_=rowsums[pair][:])
 
         def gain_of(pair):
             j = pairs[pair][1]
@@ -391,6 +389,12 @@ def tile_multiheadattentionlayer_pa_kernel(
             nc.vector.bn_aggr(out=means[t][:], in_=stats[t][:].rearrange("p h s -> p (h s)"))
 
         def rstd_of(t):
+            if t == (B - 1, TILES - 1):
+                rstds[t] = small.tile([P, 1], F32, name="rstd")
+                nc.scalar.activation(
+                    out=rstds[t][:], in_=means[t][:, 1:2], func=ACT.Abs_reciprocal_sqrt, bias=LN_EPS
+                )
+                return
             var_eps = small.tile([P, 1], F32, name="var_eps")
             nc.gpsimd.tensor_single_scalar(var_eps[:], means[t][:, 1:2], LN_EPS, op=ALU.add)
             rstds[t] = small.tile([P, 1], F32, name="rstd")
@@ -513,15 +517,10 @@ def tile_multiheadattentionlayer_pa_kernel(
             if s == 8:
                 for g in range(K_PASSES):
                     quantise_keys(1, g)
-            take = 2 if s < n_pairs + 3 else 4
+            take = 2
             for function, t, part in vector_ln[:take]:
                 function(t, part)
             vector_ln = vector_ln[take:]
-            for item in filled:
-                if item[0] in ("k", "q"):
-                    empty_heads(item)
-                elif item[0] == "x":
-                    empty_keys(item)
             if s + 1 < n_pairs:
                 shift_of(s + 1)
             take = 2
@@ -532,6 +531,11 @@ def tile_multiheadattentionlayer_pa_kernel(
                     vector_ln += [(centre, t, 0), (centre, t, 1)]
                 elif function is rstd_from_squares:
                     vector_ln += [(scale_and_store, t, 0), (scale_and_store, t, 1)]
+            for item in filled:
+                if item[0] in ("k", "q"):
+                    empty_heads(item)
+                elif item[0] == "x":
+                    empty_keys(item)
             if 0 <= s - 2 < n_pairs:
                 multiply(s - 2)
             filled = []
@@ -543,6 +547,9 @@ def tile_multiheadattentionlayer_pa_kernel(
             scalar_prep = scalar_prep[take:]
             for item in filled:
                 tensor_part[item[0]](item)
+
+            if s == n_pairs:
+                nc.scalar.activation(out=warm_out[:], in_=warm[:], func=ACT.Abs_reciprocal_sqrt)
 
             if 1 <= s < 5:
                 mask_on_vector(s - 1, 0)

@@ -272,14 +272,17 @@ def tile_multiheadattentionlayer_pa_kernel(
         def exponentiate(pair, i):
             if i == 0:
                 es[pair] = work.tile([P, 2, S], BF16, name="e")
-                rowsums[pair] = small.tile([P, 2], F32, name="rowsum")
+                if pair % 2 == 0:
+                    rowsums[pair] = small.tile([P, 4], F32, name="rowsum")
+                else:
+                    rowsums[pair] = rowsums[pair - 1]
             nc.scalar.activation(
                 out=es[pair][:, i, :],
                 in_=scores[pair, i][:],
                 func=ACT.Exp,
                 bias=shifts[pair][:, i : i + 1],
                 scale=SCORE_SCALE,
-                accum_out=rowsums[pair][:, i : i + 1],
+                accum_out=rowsums[pair][:, 2 * (pair % 2) + i : 2 * (pair % 2) + i + 1],
             )
 
         def transpose_e(pair, i):
@@ -320,13 +323,14 @@ def tile_multiheadattentionlayer_pa_kernel(
                 )
 
         def reciprocal_of(pair):
-            recips[pair] = small.tile([P, 2], F32, name="recip")
-            nc.vector.reciprocal(out=recips[pair][:], in_=rowsums[pair][:])
+            recip = small.tile([P, 4], F32, name="recip")
+            nc.vector.reciprocal(out=recip[:], in_=rowsums[pair][:])
+            recips[pair - 1], recips[pair] = recip[:, 0:2], recip[:, 2:4]
 
         def gain_of(pair):
             j = pairs[pair][1]
             gains[pair] = small.tile([P, 2], F32, name="gain")
-            nc.gpsimd.tensor_tensor(out=gains[pair][:], in0=recips[pair][:], in1=mask01[:, j, :], op=ALU.mult)
+            nc.gpsimd.tensor_tensor(out=gains[pair][:], in0=recips[pair], in1=mask01[:, j, :], op=ALU.mult)
 
         def residual(pair, i):
             b, j, h0 = pairs[pair]
@@ -493,6 +497,8 @@ def tile_multiheadattentionlayer_pa_kernel(
                 transpose_e(s, 1)
             if s + 2 < n_pairs:
                 score(s + 2, 1)
+            if dividing and s >= n_pairs:
+                quantise(s - 2)
             if ahead:
                 row_max(s + 1, 0)
             if ahead:
@@ -503,11 +509,11 @@ def tile_multiheadattentionlayer_pa_kernel(
                 residual(s - 3, 1)
             for item in biased:
                 relu(item)
-            if dividing:
+            if dividing and s < n_pairs:
                 quantise(s - 2)
             for item in biased:
                 quantise_values(item)
-            if 0 <= s - 1 < n_pairs:
+            if 0 <= s - 1 < n_pairs and s % 2 == 0:
                 reciprocal_of(s - 1)
             if dividing:
                 gain_of(s - 2)

@@ -76,8 +76,8 @@ def tile_multiheadattentionlayer_pa_kernel(
         nc.vector.memset(w_scales[:].rearrange("p g n -> p (g n)").bitcast(I32), 0)
         nc.vector.memset(bv_row[:], 0.0)
 
-        load_k(0, slice(0, HALF))
-        load_q(0, slice(0, HALF))
+        load_k(0, slice(0, HALF // 2))
+        load_q(0, slice(0, HALF // 2))
         for quad in range(4):
             nc.sync.dma_start(
                 out=w_scales[32 * quad : 32 * quad + 4, :, :].bitcast(I32),
@@ -85,16 +85,19 @@ def tile_multiheadattentionlayer_pa_kernel(
             )
         nc.sync.dma_start(out=bv_row[0:1, :], in_=bv.rearrange("(o n) -> o n", o=1))
         load_keys(0)
+        load_k(0, slice(HALF // 2, HALF))
+        load_q(0, slice(HALF // 2, HALF))
         for g in range(K_PASSES):
             nc.sync.dma_start(
                 out=w_codes[:, g, :].bitcast(I32),
                 in_=Wv_words[g].rearrange("p n t -> p (n t)").bitcast(I32),
             )
-        for slots in (slice(0, 2), slice(2, 4)):
-            for b in range(B):
-                load_x(b, slots)
+        for b in range(B):
+            load_x(b, slice(0, 2))
         load_k(0, slice(HALF, D))
         load_q(0, slice(HALF, D))
+        for b in range(B):
+            load_x(b, slice(2, 4))
         load_keys(1)
         load_k(1, slice(0, D))
         load_q(1, slice(0, D))
@@ -129,7 +132,8 @@ def tile_multiheadattentionlayer_pa_kernel(
         def tensor_heads(item):
             kind, b, h0 = item
             source = k_sb[b] if kind == "k" else q_sb[b]
-            banks[item] = psum_p.tile([P, 2, TILES, P], BF16, tag="prep", name="headsT")
+            pool, tag = (psum_o, "o_ps") if item == ("k", 0, 2) else (psum_p, "prep")
+            banks[item] = pool.tile([P, 2, TILES, P], BF16, tag=tag, name="headsT")
             for i in range(2):
                 for j in range(TILES):
                     nc.tensor.transpose(
@@ -144,10 +148,7 @@ def tile_multiheadattentionlayer_pa_kernel(
         def tensor_keys(item):
             kind, b, j = item
             keys_words = keys_sb[b][:, j, :].bitcast(F32)
-            if b == 0 and j >= 2:
-                pool, tag = ((psum_t, "eT"), (psum_o, "o_ps"))[j - 2]
-            else:
-                pool, tag = psum_p, "prep"
+            pool, tag = (psum_t, "eT") if item == ("x", 0, 2) else (psum_p, "prep")
             banks[item] = pool.tile([P, K_PASSES, 2, P], F32, tag=tag, name="keysT")
             for g in range(K_PASSES):
                 for u in range(2):
@@ -157,7 +158,7 @@ def tile_multiheadattentionlayer_pa_kernel(
 
         def empty_keys(item):
             kind, b, j = item
-            copy = nc.vector.tensor_copy if b == 0 and j % 2 == 0 else nc.scalar.copy
+            copy = nc.vector.tensor_copy if b == 0 else nc.scalar.copy
             copy(
                 out=keys_grouped[b][:].bitcast(F32)[:, :, j * P : (j + 1) * P, :],
                 in_=banks[item][:].rearrange("p g u q -> p g q u"),
@@ -439,15 +440,15 @@ def tile_multiheadattentionlayer_pa_kernel(
 
         spare = psum_o.tile([P, HALF], F32, name="o_ps")
 
-        def keep_warm():
-            nc.tensor.matmul(spare[:], lhsT=ones[:], rhs=zeros[:], start=True, stop=True)
+        def keep_warm(times):
+            for i in range(times):
+                nc.tensor.matmul(spare[:], lhsT=ones[:], rhs=zeros[:], start=True, stop=True)
 
-        for i in range(4):
-            keep_warm()
+        keep_warm(5)
         for kind in ("k", "q"):
             tensor_heads((kind, 0, 0))
             empty_heads((kind, 0, 0))
-            keep_warm()
+            keep_warm(1)
         for c in range(2):
             bv_ps = psum_p.tile([P, HALF], F32, tag="prep", name="bv_ps")
             nc.tensor.matmul(
@@ -457,12 +458,19 @@ def tile_multiheadattentionlayer_pa_kernel(
         for pair in range(2):
             for i in range(2):
                 score(pair, i)
-        for pair in range(2):
-            for i in range(2):
-                row_max(pair, i)
-        for j in range(TILES):
+        for i in range(2):
+            row_max(0, i)
+        for j in range(2):
             tensor_keys(("x", 0, j))
             empty_keys(("x", 0, j))
+        keep_warm(1)
+        tensor_keys(("x", 0, 2))
+        keep_warm(1)
+        for i in range(2):
+            row_max(1, i)
+        empty_keys(("x", 0, 2))
+        tensor_keys(("x", 0, 3))
+        empty_keys(("x", 0, 3))
         first = [(kind, 0, 2) for kind in ("k", "q")]
         for item in first:
             tensor_heads(item)

@@ -243,7 +243,7 @@ def tile_multiheadattentionlayer_pa_kernel(
         def score(pair, i):
             b, j, h0 = pairs[pair]
             scores[pair, i] = psum_s.tile([P, S], F32, name="s_ps")
-            if pair >= 2 and i == 0:
+            if pair >= 16 and i == 0:
                 nc.tensor.matmul_mx(
                     out=scores[pair, i][:, 0:512],
                     lhsT=w_codes[:, 0, 0:P].bitcast(FP8X4),

@@ -230,6 +230,8 @@ def tile_multiheadattentionlayer_pa_kernel(
             nc.scalar.activation(
                 out=abs_x[:], in_=x_sb[bb][:, j, :], func=ACT.Abs, accum_out=abs_sum[:, j, bb : bb + 1]
             )
+
+        def compare_mask(j, bb):
             nc.vector.tensor_single_scalar(mask01[:, j, bb : bb + 1], abs_sum[:, j, bb : bb + 1], 0.0, op=ALU.is_gt)
 
         pairs = []
@@ -238,7 +240,7 @@ def tile_multiheadattentionlayer_pa_kernel(
         n_pairs = len(pairs)
         QUARTER = D // 4
         scores, rowmaxs, shifts, rowsums, es, eTs, e_groupeds, quantised, outputs = {}, {}, {}, {}, {}, {}, {}, {}, {}
-        recips, gains, ys, stats, means, neg_means, sums, rstds, normeds = {}, {}, {}, {}, {}, {}, {}, {}, {}
+        recips, gains, ys, stats, means, neg_means, rstds, normeds = {}, {}, {}, {}, {}, {}, {}, {}
 
         def score(pair, i):
             b, j, h0 = pairs[pair]
@@ -310,7 +312,8 @@ def tile_multiheadattentionlayer_pa_kernel(
         def multiply(pair):
             b, j, h0 = pairs[pair]
             e_codes, e_scales = quantised[pair]
-            outputs[pair] = psum_o.tile([P, 2, DH], F32, name="o_ps")
+            pool, tag = (psum_o, "o_ps") if pair < n_pairs - 2 else (psum_p, "prep")
+            outputs[pair] = pool.tile([P, 2, DH], F32, tag=tag, name="o_ps")
             for i in range(2):
                 cols = slice((h0 + i) * DH, (h0 + i + 1) * DH)
                 nc.tensor.matmul_mx(
@@ -347,41 +350,27 @@ def tile_multiheadattentionlayer_pa_kernel(
                 op1=ALU.add,
             )
 
-        def sum_y(t, half):
-            if half == 0:
-                sums[t] = small.tile([P, 4], F32, name="sums")
-            unused = stage.tile([P, HALF], BF16, name="unused")
-            nc.scalar.activation(
-                out=unused[:],
-                in_=ys[t][:, half * HALF : (half + 1) * HALF],
-                func=ACT.Identity,
-                accum_out=sums[t][:, half : half + 1],
-            )
-
-        def mean_of(t, part):
-            unused = small.tile([P, 2], F32, name="unused2")
+        def neg_mean_of(t, part):
             neg_means[t] = small.tile([P, 1], F32, name="neg_mean")
+            unused = stage.tile([P, D], BF16, name="unused")
             nc.scalar.activation(
-                out=unused[:], in_=sums[t][:, 0:2], func=ACT.Identity, scale=-1.0 / D, accum_out=neg_means[t][:]
+                out=unused[:], in_=ys[t][:], func=ACT.Identity, scale=-1.0 / D, accum_out=neg_means[t][:]
             )
 
-        def sum_squares(t, half):
-            unused = stage.tile([P, HALF], BF16, name="unused")
+        def rstd_by_scalar(t, part):
+            squares = small.tile([P, 1], F32, name="squares")
+            unused = stage.tile([P, D], BF16, name="unused")
             nc.scalar.activation(
-                out=unused[:],
-                in_=ys[t][:, half * HALF : (half + 1) * HALF],
-                func=ACT.Square,
-                bias=neg_means[t][:],
-                accum_out=sums[t][:, 2 + half : 3 + half],
-            )
-
-        def rstd_from_squares(t, part):
-            unused = small.tile([P, 2], F32, name="unused2")
-            var_eps = small.tile([P, 1], F32, name="var_eps")
-            nc.scalar.activation(
-                out=unused[:], in_=sums[t][:, 2:4], func=ACT.Identity, scale=1.0 / D, bias=LN_EPS / 2, accum_out=var_eps[:]
+                out=unused[:], in_=ys[t][:], func=ACT.Square, bias=neg_means[t][:], accum_out=squares[:]
             )
             rstds[t] = small.tile([P, 1], F32, name="rstd")
+            if t == (B - 1, TILES - 2):
+                nc.scalar.activation(
+                    out=rstds[t][:], in_=squares[:], func=ACT.Abs_reciprocal_sqrt, scale=1.0 / D, bias=LN_EPS
+                )
+                return
+            var_eps = small.tile([P, 1], F32, name="var_eps")
+            nc.gpsimd.tensor_scalar(var_eps[:], squares[:], 1.0 / D, LN_EPS, op0=ALU.mult, op1=ALU.add)
             nc.gpsimd.tensor_tensor(out=rstds[t][:], in0=var_eps[:], in1=neg_half[:], op=ALU.pow)
 
         def statistics(t, quarter):
@@ -394,16 +383,8 @@ def tile_multiheadattentionlayer_pa_kernel(
             nc.vector.bn_aggr(out=means[t][:], in_=stats[t][:].rearrange("p h s -> p (h s)"))
 
         def rstd_of(t):
-            if t == (B - 1, TILES - 1):
-                rstds[t] = small.tile([P, 1], F32, name="rstd")
-                nc.scalar.activation(
-                    out=rstds[t][:], in_=means[t][:, 1:2], func=ACT.Abs_reciprocal_sqrt, bias=LN_EPS
-                )
-                return
-            var_eps = small.tile([P, 1], F32, name="var_eps")
-            nc.gpsimd.tensor_single_scalar(var_eps[:], means[t][:, 1:2], LN_EPS, op=ALU.add)
             rstds[t] = small.tile([P, 1], F32, name="rstd")
-            nc.gpsimd.tensor_tensor(out=rstds[t][:], in0=var_eps[:], in1=neg_half[:], op=ALU.pow)
+            nc.scalar.activation(out=rstds[t][:], in_=means[t][:, 1:2], func=ACT.Abs_reciprocal_sqrt, bias=LN_EPS)
 
         def store(t, half):
             b, j = t
@@ -454,7 +435,7 @@ def tile_multiheadattentionlayer_pa_kernel(
             nc.tensor.matmul(
                 bv_ps[:], lhsT=ones[:], rhs=bv_row[:, c * HALF : (c + 1) * HALF], start=True, stop=True
             )
-            nc.vector.tensor_copy(out=bv_bc[:, c * HALF : (c + 1) * HALF], in_=bv_ps[:])
+            nc.scalar.copy(out=bv_bc[:, c * HALF : (c + 1) * HALF], in_=bv_ps[:])
         for pair in range(2):
             for i in range(2):
                 score(pair, i)
@@ -484,46 +465,37 @@ def tile_multiheadattentionlayer_pa_kernel(
         scalar_prep += [(kind, 1, h0) for h0 in range(0, H, 2) for kind in ("k", "q")]
         vector_prep = [("v", b, h) for b in range(B) for h in range(H)]
 
-        VECTOR_TILES = ((1, 2), (1, 3))
+        VECTOR_TILES = ((1, 3),)
         vector_ln, scalar_ln = [], []
-        filled, biased, complete = first, [], []
-        for s in range(n_pairs + 12):
-            ahead = 0 < s and s + 1 < n_pairs
-            dividing = 0 <= s - 2 < n_pairs
-            finishing = 0 <= s - 3 < n_pairs
-            if s < n_pairs:
-                exponentiate(s, 0)
-            if 0 <= s - 1 < n_pairs:
+        filled, biased = first, []
+        for s in range(n_pairs):
+            exponentiate(s, 0)
+            if s >= 1:
                 regroup(s - 1)
-            if s < n_pairs:
-                exponentiate(s, 1)
+            exponentiate(s, 1)
             if s + 2 < n_pairs:
                 score(s + 2, 0)
-            if s < n_pairs:
-                transpose_e(s, 0)
-            if s < n_pairs:
-                transpose_e(s, 1)
+            transpose_e(s, 0)
+            transpose_e(s, 1)
             if s + 2 < n_pairs:
                 score(s + 2, 1)
-            if dividing and s >= n_pairs:
-                quantise(s - 2)
-            if ahead:
+            if s >= 2 and s % 2 == 0:
+                reciprocal_of(s - 1)
+            if 0 < s and s + 1 < n_pairs:
                 row_max(s + 1, 0)
-            if ahead:
                 row_max(s + 1, 1)
-            if finishing:
+            if s >= 3:
                 residual(s - 3, 0)
-            if finishing:
                 residual(s - 3, 1)
             for item in biased:
                 relu(item)
-            if dividing and s < n_pairs:
+            if s >= 2:
                 quantise(s - 2)
             for item in biased:
                 quantise_values(item)
-            if 0 <= s - 1 < n_pairs and s % 2 == 0:
-                reciprocal_of(s - 1)
-            if dividing:
+            if 2 <= s < 6:
+                compare_mask(s - 2, 1)
+            if s >= 2:
                 gain_of(s - 2)
             biased = [item for item in filled if item[0] == "v"]
             for item in biased:
@@ -531,55 +503,69 @@ def tile_multiheadattentionlayer_pa_kernel(
             if s == 8:
                 for g in range(K_PASSES):
                     quantise_keys(1, g)
-            take = 2
-            for function, t, part in vector_ln[:take]:
-                function(t, part)
-            vector_ln = vector_ln[take:]
-            if s + 1 < n_pairs:
-                shift_of(s + 1)
-            take = 2
-            pieces, scalar_ln = scalar_ln[:take], scalar_ln[take:]
+            pieces, vector_ln = vector_ln[:2], vector_ln[2:]
             for function, t, part in pieces:
                 function(t, part)
-                if function is mean_of:
-                    vector_ln += [(centre, t, 0), (centre, t, 1)]
-                elif function is rstd_from_squares:
-                    vector_ln += [(scale_and_store, t, 0), (scale_and_store, t, 1)]
+            if s + 1 < n_pairs:
+                shift_of(s + 1)
+            pieces, scalar_ln = scalar_ln[:1], scalar_ln[1:]
+            for function, t, part in pieces:
+                function(t, part)
+                apply = centre if function is neg_mean_of else scale_and_store
+                vector_ln += [(apply, t, 0), (apply, t, 1)]
             for item in filled:
                 if item[0] in ("k", "q"):
                     empty_heads(item)
                 elif item[0] == "x":
                     empty_keys(item)
-            if 0 <= s - 2 < n_pairs:
+            if s >= 2:
                 multiply(s - 2)
-            filled = []
             take = 2 if s == 0 else 0 if s in (7, 8) else 1
-            filled += vector_prep[:take]
-            vector_prep = vector_prep[take:]
+            filled, vector_prep = vector_prep[:take], vector_prep[take:]
             take = 1 if s > 0 else 0
-            filled += scalar_prep[:take]
+            filled = filled + scalar_prep[:take]
             scalar_prep = scalar_prep[take:]
             for item in filled:
                 tensor_part[item[0]](item)
 
-            if s == n_pairs:
-                nc.scalar.activation(out=warm_out[:], in_=warm[:], func=ACT.Abs_reciprocal_sqrt)
-
             if 1 <= s < 5:
                 mask_on_vector(s - 1, 0)
                 mask_on_scalar(s - 1, 1)
-            if finishing:
-                t, h0 = pairs[s - 3][:2], pairs[s - 3][2]
-                if t in VECTOR_TILES:
-                    statistics(t, h0 // 2)
-                    if h0 == H - 2:
-                        aggregate(t)
-                        rstd_of(t)
-                        vector_ln += [(centre, t, 0), (centre, t, 1)]
-                        vector_ln += [(scale_and_store, t, 0), (scale_and_store, t, 1)]
-                elif h0 == 2:
-                    scalar_ln.append((sum_y, t, 0))
-                elif h0 == H - 2:
-                    scalar_ln += [(sum_y, t, 1), (mean_of, t, None), (sum_squares, t, 0), (sum_squares, t, 1)]
-                    scalar_ln.append((rstd_from_squares, t, None))
-        assert not (vector_ln or scalar_ln or scalar_prep or vector_prep or filled or biased)
+            if s >= 3:
+                b, j, h0 = pairs[s - 3]
+                if (b, j) in VECTOR_TILES:
+                    statistics((b, j), h0 // 2)
+                elif h0 == H - 2 and (b, j) != (B - 1, TILES - 2):
+                    scalar_ln += [(neg_mean_of, (b, j), None), (rstd_by_scalar, (b, j), None)]
+        assert not (scalar_prep or vector_prep or filled or biased or scalar_ln or vector_ln)
+
+        last = n_pairs - 1
+        regroup(last)
+        nearly, final = (B - 1, TILES - 2), (B - 1, TILES - 1)
+        neg_mean_of(nearly, None)
+        rstd_by_scalar(nearly, None)
+        reciprocal_of(last)
+        for pair in (last - 1, last):
+            gain_of(pair)
+        quantise(last - 1)
+        multiply(last - 1)
+        for i in range(2):
+            residual(last - 2, i)
+        statistics(final, 1)
+        for i in range(2):
+            residual(last - 1, i)
+        quantise(last)
+        multiply(last)
+        statistics(final, 2)
+        for i in range(2):
+            residual(last, i)
+        centre(nearly, 0)
+        statistics(final, 3)
+        centre(nearly, 1)
+        aggregate(final)
+        rstd_of(final)
+        for half in range(2):
+            centre(final, half)
+        for t in (nearly, final):
+            for half in range(2):
+                scale_and_store(t, half)

@@ -69,21 +69,26 @@ def tile_multiheadattentionlayer_pa_kernel(
                     in_=keys[b].rearrange("(u p e) d -> p u e d", u=2, e=2)[:, u, :, :],
                 )
 
+        warm = keep.tile([P, 1], F32)
+        nc.vector.memset(warm[:], 1.0)
+        warm_out = keep.tile([P, 1], F32)
+        nc.scalar.activation(out=warm_out[:], in_=warm[:], func=ACT.Exp)
         ones = keep.tile([P, P], BF16)
         nc.vector.memset(ones[:], 1.0)
         zeros = keep.tile([P, HALF], BF16)
         nc.vector.memset(zeros[:], 0.0)
-        nc.vector.memset(w_scales[:].rearrange("p g n -> p (g n)").bitcast(I32), 0)
         nc.vector.memset(bv_row[:], 0.0)
+        nc.vector.memset(w_scales[:].rearrange("p g n -> p (g n)").bitcast(I32), 0)
 
         load_k(0, slice(0, HALF // 2))
         load_q(0, slice(0, HALF // 2))
+        nc.sync.dma_start(out=bv_row[0:1, :], in_=bv.rearrange("(o n) -> o n", o=1))
+        load_x(0, slice(0, 1))
         for quad in range(4):
             nc.sync.dma_start(
                 out=w_scales[32 * quad : 32 * quad + 4, :, :].bitcast(I32),
                 in_=Wv_scales[:, 4 * quad : 4 * quad + 4, :].rearrange("g r n -> r g n").bitcast(I32),
             )
-        nc.sync.dma_start(out=bv_row[0:1, :], in_=bv.rearrange("(o n) -> o n", o=1))
         load_keys(0)
         load_k(0, slice(HALF // 2, HALF))
         load_q(0, slice(HALF // 2, HALF))
@@ -92,8 +97,9 @@ def tile_multiheadattentionlayer_pa_kernel(
                 out=w_codes[:, g, :].bitcast(I32),
                 in_=Wv_words[g].rearrange("p n t -> p (n t)").bitcast(I32),
             )
+        load_x(1, slice(0, 1))
         for b in range(B):
-            load_x(b, slice(0, 2))
+            load_x(b, slice(1, 2))
         load_k(0, slice(HALF, D))
         load_q(0, slice(HALF, D))
         for b in range(B):
@@ -110,10 +116,6 @@ def tile_multiheadattentionlayer_pa_kernel(
         make_identity(nc, ident_f32[:])
         neg_half = keep.tile([P, 1], F32)
         nc.gpsimd.memset(neg_half[:], -0.5)
-        warm = keep.tile([P, 1], F32)
-        nc.vector.memset(warm[:], 1.0)
-        warm_out = keep.tile([P, 1], F32)
-        nc.scalar.activation(out=warm_out[:], in_=warm[:], func=ACT.Exp)
 
         qT = keep.tile([P, B, H, TILES, P], BF16)
         kT = keep.tile([P, B, H, TILES, P], BF16)
@@ -143,7 +145,8 @@ def tile_multiheadattentionlayer_pa_kernel(
         def empty_heads(item):
             kind, b, h0 = item
             target = kT if kind == "k" else qT
-            nc.scalar.copy(out=target[:, b, h0 : h0 + 2, :, :], in_=banks[item][:])
+            copy = nc.vector.tensor_copy if item == ("q", 0, 0) else nc.scalar.copy
+            copy(out=target[:, b, h0 : h0 + 2, :, :], in_=banks[item][:])
 
         def tensor_keys(item):
             kind, b, j = item
@@ -158,11 +161,13 @@ def tile_multiheadattentionlayer_pa_kernel(
 
         def empty_keys(item):
             kind, b, j = item
-            copy = nc.vector.tensor_copy if b == 0 else nc.scalar.copy
+            copy = nc.vector.tensor_copy if (b, j) in VECTOR_KEYS else nc.scalar.copy
             copy(
                 out=keys_grouped[b][:].bitcast(F32)[:, :, j * P : (j + 1) * P, :],
                 in_=banks[item][:].rearrange("p g u q -> p g q u"),
             )
+
+        VECTOR_KEYS = ((0, 2), (0, 3))
 
         def quantise_keys(b, g):
             nc.vector.quantize_mx(
@@ -242,10 +247,12 @@ def tile_multiheadattentionlayer_pa_kernel(
         scores, rowmaxs, shifts, rowsums, es, eTs, e_groupeds, quantised, outputs = {}, {}, {}, {}, {}, {}, {}, {}, {}
         recips, gains, ys, stats, means, neg_means, rstds, normeds = {}, {}, {}, {}, {}, {}, {}, {}
 
+        V_PAUSE = (7, 8)
+
         def score(pair, i):
             b, j, h0 = pairs[pair]
             scores[pair, i] = psum_s.tile([P, S], F32, name="s_ps")
-            if pair >= 16 and i == 0:
+            if i == 0 and (pair - 2 in V_PAUSE or pair - 2 >= B * H):
                 nc.tensor.matmul_mx(
                     out=scores[pair, i][:, 0:512],
                     lhsT=w_codes[:, 0, 0:P].bitcast(FP8X4),
@@ -290,7 +297,7 @@ def tile_multiheadattentionlayer_pa_kernel(
 
         def transpose_e(pair, i):
             if i == 0:
-                eTs[pair] = psum_t.tile([P, 2, 2, P], F32, name="eT")
+                eTs[pair] = psum_t.tile([P, 2, 2, P], F32, tag="eT", name="eT")
             e_words = es[pair][:, i, :].bitcast(F32)
             for u in range(2):
                 nc.tensor.transpose(eTs[pair][:, i, u, :], e_words[:, u * P : (u + 1) * P], ident_f32[:])
@@ -386,17 +393,19 @@ def tile_multiheadattentionlayer_pa_kernel(
             rstds[t] = small.tile([P, 1], F32, name="rstd")
             nc.scalar.activation(out=rstds[t][:], in_=means[t][:, 1:2], func=ACT.Abs_reciprocal_sqrt, bias=LN_EPS)
 
+        PARTS = (slice(0, HALF), slice(HALF, D), slice(0, D))
+
         def store(t, half):
             b, j = t
-            cols = slice(half * HALF, (half + 1) * HALF)
+            cols = PARTS[half]
             nc.sync.dma_start(
                 out=out[b].rearrange("(p j) d -> p j d", j=TILES)[:, j, cols], in_=normeds[t][:, cols]
             )
 
         def centre(t, half):
-            if half == 0:
+            if half != 1:
                 normeds[t] = work.tile([P, D], F32, name="normed")
-            cols = slice(half * HALF, (half + 1) * HALF)
+            cols = PARTS[half]
             by_vector = t in VECTOR_TILES
             nc.vector.scalar_tensor_tensor(
                 out=normeds[t][:, cols],
@@ -408,7 +417,7 @@ def tile_multiheadattentionlayer_pa_kernel(
             )
 
         def scale_and_store(t, half):
-            cols = slice(half * HALF, (half + 1) * HALF)
+            cols = PARTS[half]
             nc.vector.scalar_tensor_tensor(
                 out=normeds[t][:, cols],
                 in0=normeds[t][:, cols],
@@ -429,9 +438,9 @@ def tile_multiheadattentionlayer_pa_kernel(
         for kind in ("k", "q"):
             tensor_heads((kind, 0, 0))
             empty_heads((kind, 0, 0))
-            keep_warm(1)
         for c in range(2):
-            bv_ps = psum_p.tile([P, HALF], F32, tag="prep", name="bv_ps")
+            pool, tag = ((psum_t, "eT"), (psum_p, "prep"))[c]
+            bv_ps = pool.tile([P, HALF], F32, tag=tag, name="bv_ps")
             nc.tensor.matmul(
                 bv_ps[:], lhsT=ones[:], rhs=bv_row[:, c * HALF : (c + 1) * HALF], start=True, stop=True
             )
@@ -441,23 +450,18 @@ def tile_multiheadattentionlayer_pa_kernel(
                 score(pair, i)
         for i in range(2):
             row_max(0, i)
-        for j in range(2):
-            tensor_keys(("x", 0, j))
-            empty_keys(("x", 0, j))
-        keep_warm(1)
-        tensor_keys(("x", 0, 2))
-        keep_warm(1)
+        mask_on_vector(0, 0)
         for i in range(2):
             row_max(1, i)
-        empty_keys(("x", 0, 2))
-        tensor_keys(("x", 0, 3))
-        empty_keys(("x", 0, 3))
+        shift_of(0)
+        for j in range(TILES):
+            tensor_keys(("x", 0, j))
+            empty_keys(("x", 0, j))
+            keep_warm(1)
         first = [(kind, 0, 2) for kind in ("k", "q")]
-        for item in first:
-            tensor_heads(item)
+        tensor_heads(first[0])
         for g in range(K_PASSES):
             quantise_keys(0, g)
-        shift_of(0)
 
         scalar_prep = [(kind, 0, 4) for kind in ("k", "q")]
         scalar_prep += [("x", 1, j) for j in range(TILES)]
@@ -477,6 +481,8 @@ def tile_multiheadattentionlayer_pa_kernel(
                 score(s + 2, 0)
             transpose_e(s, 0)
             transpose_e(s, 1)
+            if s == 0:
+                tensor_heads(first[1])
             if s + 2 < n_pairs:
                 score(s + 2, 1)
             if s >= 2 and s % 2 == 0:
@@ -503,7 +509,7 @@ def tile_multiheadattentionlayer_pa_kernel(
             if s == 8:
                 for g in range(K_PASSES):
                     quantise_keys(1, g)
-            pieces, vector_ln = vector_ln[:2], vector_ln[2:]
+            pieces, vector_ln = vector_ln[:1], vector_ln[1:]
             for function, t, part in pieces:
                 function(t, part)
             if s + 1 < n_pairs:
@@ -512,7 +518,7 @@ def tile_multiheadattentionlayer_pa_kernel(
             for function, t, part in pieces:
                 function(t, part)
                 apply = centre if function is neg_mean_of else scale_and_store
-                vector_ln += [(apply, t, 0), (apply, t, 1)]
+                vector_ln.append((apply, t, 2))
             for item in filled:
                 if item[0] in ("k", "q"):
                     empty_heads(item)
@@ -520,7 +526,7 @@ def tile_multiheadattentionlayer_pa_kernel(
                     empty_keys(item)
             if s >= 2:
                 multiply(s - 2)
-            take = 2 if s == 0 else 0 if s in (7, 8) else 1
+            take = 2 if s == 0 else 0 if s in V_PAUSE else 1
             filled, vector_prep = vector_prep[:take], vector_prep[take:]
             take = 1 if s > 0 else 0
             filled = filled + scalar_prep[:take]
@@ -529,7 +535,8 @@ def tile_multiheadattentionlayer_pa_kernel(
                 tensor_part[item[0]](item)
 
             if 1 <= s < 5:
-                mask_on_vector(s - 1, 0)
+                if s > 1:
+                    mask_on_vector(s - 1, 0)
                 mask_on_scalar(s - 1, 1)
             if s >= 3:
                 b, j, h0 = pairs[s - 3]

@@ -90,6 +90,7 @@ def tile_multiheadattentionlayer_pa_kernel(
                 in_=Wv_scales[:, 4 * quad : 4 * quad + 4, :].rearrange("g r n -> r g n").bitcast(I32),
             )
         load_keys(0)
+        load_x(1, slice(0, 1))
         load_k(0, slice(HALF // 2, HALF))
         load_q(0, slice(HALF // 2, HALF))
         for g in range(K_PASSES):
@@ -97,7 +98,6 @@ def tile_multiheadattentionlayer_pa_kernel(
                 out=w_codes[:, g, :].bitcast(I32),
                 in_=Wv_words[g].rearrange("p n t -> p (n t)").bitcast(I32),
             )
-        load_x(1, slice(0, 1))
         for b in range(B):
             load_x(b, slice(1, 2))
         load_k(0, slice(HALF, D))
@@ -343,10 +343,15 @@ def tile_multiheadattentionlayer_pa_kernel(
             gains[pair] = small.tile([P, 2], F32, name="gain")
             nc.gpsimd.tensor_tensor(out=gains[pair][:], in0=recips[pair], in1=mask01[:, j, :], op=ALU.mult)
 
+        SUMMED_TILES = ((1, 0),)
+        sums = {}
+
         def residual(pair, i):
             b, j, h0 = pairs[pair]
             if h0 == 0 and i == 0:
                 ys[b, j] = rows.tile([P, D], F32, name="y")
+                if (b, j) in SUMMED_TILES:
+                    sums[b, j] = small.tile([P, H], F32, name="sums")
             cols = slice((h0 + i) * DH, (h0 + i + 1) * DH)
             nc.vector.scalar_tensor_tensor(
                 out=ys[b, j][:, cols],
@@ -355,13 +360,15 @@ def tile_multiheadattentionlayer_pa_kernel(
                 in1=x_sb[b][:, j, cols],
                 op0=ALU.mult,
                 op1=ALU.add,
+                accum_out=sums[b, j][:, h0 + i : h0 + i + 1] if (b, j) in SUMMED_TILES else None,
             )
 
         def neg_mean_of(t, part):
             neg_means[t] = small.tile([P, 1], F32, name="neg_mean")
+            source = sums[t] if t in SUMMED_TILES else ys[t]
             unused = stage.tile([P, D], BF16, name="unused")
             nc.scalar.activation(
-                out=unused[:], in_=ys[t][:], func=ACT.Identity, scale=-1.0 / D, accum_out=neg_means[t][:]
+                out=unused[:, : source.shape[1]], in_=source[:], func=ACT.Identity, scale=-1.0 / D, accum_out=neg_means[t][:]
             )
 
         def rstd_by_scalar(t, part):
@@ -477,6 +484,8 @@ def tile_multiheadattentionlayer_pa_kernel(
             if s >= 1:
                 regroup(s - 1)
             exponentiate(s, 1)
+            if s == 0:
+                mask_on_scalar(0, 1)
             if s + 2 < n_pairs:
                 score(s + 2, 0)
             transpose_e(s, 0)
@@ -537,7 +546,7 @@ def tile_multiheadattentionlayer_pa_kernel(
             if 1 <= s < 5:
                 if s > 1:
                     mask_on_vector(s - 1, 0)
-                mask_on_scalar(s - 1, 1)
+                    mask_on_scalar(s - 1, 1)
             if s >= 3:
                 b, j, h0 = pairs[s - 3]
                 if (b, j) in VECTOR_TILES:

@@ -56,8 +56,10 @@ def tile_multiheadattentionlayer_pa_kernel(
         def load_k(b, cols):
             nc.sync.dma_start(out=k_sb[b][:, :, cols], in_=k_relu[b].rearrange("(j p) d -> p j d", j=TILES)[:, :, cols])
 
-        def load_q(b, cols):
-            nc.sync.dma_start(out=q_sb[b][:, :, cols], in_=q_relu[b].rearrange("(p j) d -> p j d", j=TILES)[:, :, cols])
+        def load_q(b, cols, slots=slice(0, TILES)):
+            nc.sync.dma_start(
+                out=q_sb[b][:, slots, cols], in_=q_relu[b].rearrange("(p j) d -> p j d", j=TILES)[:, slots, cols]
+            )
 
         def load_x(b, slots):
             nc.sync.dma_start(out=x_sb[b][:, slots, :], in_=queries[b].rearrange("(p j) d -> p j d", j=TILES)[:, slots, :])
@@ -81,7 +83,8 @@ def tile_multiheadattentionlayer_pa_kernel(
         nc.vector.memset(w_scales[:].rearrange("p g n -> p (g n)").bitcast(I32), 0)
 
         load_k(0, slice(0, HALF // 2))
-        load_q(0, slice(0, HALF // 2))
+        for slots in (slice(0, 1), slice(1, TILES)):
+            load_q(0, slice(0, HALF // 2), slots)
         nc.sync.dma_start(out=bv_row[0:1, :], in_=bv.rearrange("(o n) -> o n", o=1))
         load_x(0, slice(0, 1))
         for quad in range(4):
@@ -145,8 +148,7 @@ def tile_multiheadattentionlayer_pa_kernel(
         def empty_heads(item):
             kind, b, h0 = item
             target = kT if kind == "k" else qT
-            copy = nc.vector.tensor_copy if item == ("q", 0, 0) else nc.scalar.copy
-            copy(out=target[:, b, h0 : h0 + 2, :, :], in_=banks[item][:])
+            nc.scalar.copy(out=target[:, b, h0 : h0 + 2, :, :], in_=banks[item][:])
 
         def tensor_keys(item):
             kind, b, j = item
@@ -167,7 +169,7 @@ def tile_multiheadattentionlayer_pa_kernel(
                 in_=banks[item][:].rearrange("p g u q -> p g q u"),
             )
 
-        VECTOR_KEYS = ((0, 2), (0, 3))
+        VECTOR_KEYS = ((0, 0), (0, 1), (0, 2), (0, 3))
 
         def quantise_keys(b, g):
             nc.vector.quantize_mx(
@@ -251,7 +253,7 @@ def tile_multiheadattentionlayer_pa_kernel(
 
         def score(pair, i):
             b, j, h0 = pairs[pair]
-            scores[pair, i] = psum_s.tile([P, S], F32, name="s_ps")
+            scores[pair, i] = psum_s.tile([P, S], F32, tag="s_ps", name="s_ps")
             if i == 0 and (pair - 2 in V_PAUSE or pair - 2 >= B * H):
                 nc.tensor.matmul_mx(
                     out=scores[pair, i][:, 0:512],
@@ -341,9 +343,10 @@ def tile_multiheadattentionlayer_pa_kernel(
         def gain_of(pair):
             j = pairs[pair][1]
             gains[pair] = small.tile([P, 2], F32, name="gain")
-            nc.gpsimd.tensor_tensor(out=gains[pair][:], in0=recips[pair], in1=mask01[:, j, :], op=ALU.mult)
+            multiply_on = nc.vector if pair >= n_pairs - 4 else nc.gpsimd
+            multiply_on.tensor_tensor(out=gains[pair][:], in0=recips[pair], in1=mask01[:, j, :], op=ALU.mult)
 
-        SUMMED_TILES = ((1, 0),)
+        SUMMED_TILES = ((1, 0), (1, 2))
         sums = {}
 
         def residual(pair, i):
@@ -442,9 +445,20 @@ def tile_multiheadattentionlayer_pa_kernel(
                 nc.tensor.matmul(spare[:], lhsT=ones[:], rhs=zeros[:], start=True, stop=True)
 
         keep_warm(5)
-        for kind in ("k", "q"):
-            tensor_heads((kind, 0, 0))
-            empty_heads((kind, 0, 0))
+
+        def first_heads(source, target, pool, tag, heads, slots, copy):
+            bank = pool.tile([P, len(heads), len(slots), P], BF16, tag=tag, name="first_heads")
+            for i, h in enumerate(heads):
+                for m, j in enumerate(slots):
+                    nc.tensor.transpose(bank[:, i, m, :], source[:, j, h * DH : (h + 1) * DH], ident_bf[:])
+            copy(out=target[:, 0, heads[0] : heads[-1] + 1, slots[0] : slots[-1] + 1, :], in_=bank[:])
+
+        first_heads(k_sb[0], kT, psum_p, "prep", (0,), (0, 1, 2, 3), nc.scalar.copy)
+        first_heads(k_sb[0], kT, psum_p, "prep", (1,), (0, 1, 2, 3), nc.vector.tensor_copy)
+        first_heads(q_sb[0], qT, psum_t, "eT", (0, 1), (0,), nc.scalar.copy)
+        first_heads(q_sb[0], qT, psum_s, "s_ps", (0, 1), (1, 2, 3), nc.vector.tensor_copy)
+        for i in range(2):
+            score(0, i)
         for c in range(2):
             pool, tag = ((psum_t, "eT"), (psum_p, "prep"))[c]
             bv_ps = pool.tile([P, HALF], F32, tag=tag, name="bv_ps")
@@ -452,19 +466,24 @@ def tile_multiheadattentionlayer_pa_kernel(
                 bv_ps[:], lhsT=ones[:], rhs=bv_row[:, c * HALF : (c + 1) * HALF], start=True, stop=True
             )
             nc.scalar.copy(out=bv_bc[:, c * HALF : (c + 1) * HALF], in_=bv_ps[:])
-        for pair in range(2):
-            for i in range(2):
-                score(pair, i)
+        for i in range(2):
+            score(1, i)
         for i in range(2):
             row_max(0, i)
         mask_on_vector(0, 0)
         for i in range(2):
             row_max(1, i)
         shift_of(0)
+        for i in range(2):
+            exponentiate(0, i)
+        mask_on_scalar(0, 1)
+        shift_of(1)
+        exponentiate(1, 0)
         for j in range(TILES):
             tensor_keys(("x", 0, j))
             empty_keys(("x", 0, j))
             keep_warm(1)
+        exponentiate(1, 1)
         first = [(kind, 0, 2) for kind in ("k", "q")]
         tensor_heads(first[0])
         for g in range(K_PASSES):
@@ -480,12 +499,12 @@ def tile_multiheadattentionlayer_pa_kernel(
         vector_ln, scalar_ln = [], []
         filled, biased = first, []
         for s in range(n_pairs):
-            exponentiate(s, 0)
+            if s >= 2:
+                exponentiate(s, 0)
             if s >= 1:
                 regroup(s - 1)
-            exponentiate(s, 1)
-            if s == 0:
-                mask_on_scalar(0, 1)
+            if s >= 2:
+                exponentiate(s, 1)
             if s + 2 < n_pairs:
                 score(s + 2, 0)
             transpose_e(s, 0)
@@ -521,7 +540,7 @@ def tile_multiheadattentionlayer_pa_kernel(
             pieces, vector_ln = vector_ln[:1], vector_ln[1:]
             for function, t, part in pieces:
                 function(t, part)
-            if s + 1 < n_pairs:
+            if 0 < s and s + 1 < n_pairs:
                 shift_of(s + 1)
             pieces, scalar_ln = scalar_ln[:1], scalar_ln[1:]
             for function, t, part in pieces:
@@ -580,8 +599,9 @@ def tile_multiheadattentionlayer_pa_kernel(
         centre(nearly, 1)
         aggregate(final)
         rstd_of(final)
+        scale_and_store(nearly, 0)
         for half in range(2):
             centre(final, half)
-        for t in (nearly, final):
-            for half in range(2):
-                scale_and_store(t, half)
+        scale_and_store(nearly, 1)
+        for half in range(2):
+            scale_and_store(final, half)

@@ -346,7 +346,7 @@ def tile_multiheadattentionlayer_pa_kernel(
             multiply_on = nc.vector if pair >= n_pairs - 4 else nc.gpsimd
             multiply_on.tensor_tensor(out=gains[pair][:], in0=recips[pair], in1=mask01[:, j, :], op=ALU.mult)
 
-        SUMMED_TILES = ((1, 0), (1, 2))
+        SUMMED_TILES = ((1, 0), (1, 2), (1, 3))
         sums = {}
 
         def residual(pair, i):
@@ -381,7 +381,7 @@ def tile_multiheadattentionlayer_pa_kernel(
                 out=unused[:], in_=ys[t][:], func=ACT.Square, bias=neg_means[t][:], accum_out=squares[:]
             )
             rstds[t] = small.tile([P, 1], F32, name="rstd")
-            if t == (B - 1, TILES - 2):
+            if t in ((B - 1, TILES - 2), (B - 1, TILES - 1)):
                 nc.scalar.activation(
                     out=rstds[t][:], in_=squares[:], func=ACT.Abs_reciprocal_sqrt, scale=1.0 / D, bias=LN_EPS
                 )
@@ -389,19 +389,6 @@ def tile_multiheadattentionlayer_pa_kernel(
             var_eps = small.tile([P, 1], F32, name="var_eps")
             nc.gpsimd.tensor_scalar(var_eps[:], squares[:], 1.0 / D, LN_EPS, op0=ALU.mult, op1=ALU.add)
             nc.gpsimd.tensor_tensor(out=rstds[t][:], in0=var_eps[:], in1=neg_half[:], op=ALU.pow)
-
-        def statistics(t, quarter):
-            if quarter == 0:
-                stats[t] = small.tile([P, 4, 6], F32, name="stats")
-            nc.vector.bn_stats(out=stats[t][:, quarter, :], in_=ys[t][:, quarter * QUARTER : (quarter + 1) * QUARTER])
-
-        def aggregate(t):
-            means[t] = small.tile([P, 2], F32, name="mean_var")
-            nc.vector.bn_aggr(out=means[t][:], in_=stats[t][:].rearrange("p h s -> p (h s)"))
-
-        def rstd_of(t):
-            rstds[t] = small.tile([P, 1], F32, name="rstd")
-            nc.scalar.activation(out=rstds[t][:], in_=means[t][:, 1:2], func=ACT.Abs_reciprocal_sqrt, bias=LN_EPS)
 
         PARTS = (slice(0, HALF), slice(HALF, D), slice(0, D))
 
@@ -416,13 +403,12 @@ def tile_multiheadattentionlayer_pa_kernel(
             if half != 1:
                 normeds[t] = work.tile([P, D], F32, name="normed")
             cols = PARTS[half]
-            by_vector = t in VECTOR_TILES
             nc.vector.scalar_tensor_tensor(
                 out=normeds[t][:, cols],
                 in0=ys[t][:, cols],
-                scalar=means[t][:, 0:1] if by_vector else neg_means[t][:],
+                scalar=neg_means[t][:],
                 in1=gamma_bc[:, cols],
-                op0=ALU.subtract if by_vector else ALU.add,
+                op0=ALU.add,
                 op1=ALU.mult,
             )
 
@@ -495,7 +481,6 @@ def tile_multiheadattentionlayer_pa_kernel(
         scalar_prep += [(kind, 1, h0) for h0 in range(0, H, 2) for kind in ("k", "q")]
         vector_prep = [("v", b, h) for b in range(B) for h in range(H)]
 
-        VECTOR_TILES = ((1, 3),)
         vector_ln, scalar_ln = [], []
         filled, biased = first, []
         for s in range(n_pairs):
@@ -568,37 +553,33 @@ def tile_multiheadattentionlayer_pa_kernel(
                     mask_on_scalar(s - 1, 1)
             if s >= 3:
                 b, j, h0 = pairs[s - 3]
-                if (b, j) in VECTOR_TILES:
-                    statistics((b, j), h0 // 2)
-                elif h0 == H - 2 and (b, j) != (B - 1, TILES - 2):
+                if h0 == H - 2 and (b, j) != (B - 1, TILES - 2):
                     scalar_ln += [(neg_mean_of, (b, j), None), (rstd_by_scalar, (b, j), None)]
         assert not (scalar_prep or vector_prep or filled or biased or scalar_ln or vector_ln)
 
         last = n_pairs - 1
-        regroup(last)
         nearly, final = (B - 1, TILES - 2), (B - 1, TILES - 1)
         neg_mean_of(nearly, None)
+        nc.scalar.activation(out=warm_out[:], in_=warm[:], func=ACT.Abs_reciprocal_sqrt)
+        regroup(last)
         rstd_by_scalar(nearly, None)
         reciprocal_of(last)
+        quantise(last - 1)
         for pair in (last - 1, last):
             gain_of(pair)
-        quantise(last - 1)
         multiply(last - 1)
         for i in range(2):
             residual(last - 2, i)
-        statistics(final, 1)
         for i in range(2):
             residual(last - 1, i)
+        centre(nearly, 0)
         quantise(last)
         multiply(last)
-        statistics(final, 2)
+        centre(nearly, 1)
         for i in range(2):
             residual(last, i)
-        centre(nearly, 0)
-        statistics(final, 3)
-        centre(nearly, 1)
-        aggregate(final)
-        rstd_of(final)
+        neg_mean_of(final, None)
+        rstd_by_scalar(final, None)
         scale_and_store(nearly, 0)
         for half in range(2):
             centre(final, half)

@@ -251,6 +251,8 @@ def tile_multiheadattentionlayer_pa_kernel(
 
         V_PAUSE = (7, 8)
 
+        FREE_FROM = B * H + 3
+
         def score(pair, i):
             b, j, h0 = pairs[pair]
             scores[pair, i] = psum_s.tile([P, S], F32, tag="s_ps", name="s_ps")
@@ -299,7 +301,8 @@ def tile_multiheadattentionlayer_pa_kernel(
 
         def transpose_e(pair, i):
             if i == 0:
-                eTs[pair] = psum_t.tile([P, 2, 2, P], F32, tag="eT", name="eT")
+                pool, tag = (psum_p, "prep") if pair >= FREE_FROM and pair % 2 == 1 else (psum_t, "eT")
+                eTs[pair] = pool.tile([P, 2, 2, P], F32, tag=tag, name="eT")
             e_words = es[pair][:, i, :].bitcast(F32)
             for u in range(2):
                 nc.tensor.transpose(eTs[pair][:, i, u, :], e_words[:, u * P : (u + 1) * P], ident_f32[:])
@@ -321,7 +324,7 @@ def tile_multiheadattentionlayer_pa_kernel(
         def multiply(pair):
             b, j, h0 = pairs[pair]
             e_codes, e_scales = quantised[pair]
-            pool, tag = (psum_o, "o_ps") if pair < n_pairs - 2 else (psum_p, "prep")
+            pool, tag = (psum_p, "prep") if pair >= FREE_FROM and pair % 2 == 1 else (psum_o, "o_ps")
             outputs[pair] = pool.tile([P, 2, DH], F32, tag=tag, name="o_ps")
             for i in range(2):
                 cols = slice((h0 + i) * DH, (h0 + i + 1) * DH)
@@ -336,15 +339,22 @@ def tile_multiheadattentionlayer_pa_kernel(
                 )
 
         def reciprocal_of(pair):
-            recip = small.tile([P, 4], F32, name="recip")
-            nc.vector.reciprocal(out=recip[:], in_=rowsums[pair][:])
-            recips[pair - 1], recips[pair] = recip[:, 0:2], recip[:, 2:4]
+            recips[pair] = small.tile([P, 2, 2], F32, name="recip")
+            nc.vector.reciprocal(out=recips[pair][:].rearrange("p a i -> p (a i)"), in_=rowsums[pair][:])
 
-        def gain_of(pair):
+        def gain_of(pair, engine):
             j = pairs[pair][1]
-            gains[pair] = small.tile([P, 2], F32, name="gain")
-            multiply_on = nc.vector if pair >= n_pairs - 4 else nc.gpsimd
-            multiply_on.tensor_tensor(out=gains[pair][:], in0=recips[pair], in1=mask01[:, j, :], op=ALU.mult)
+            gain = small.tile([P, 2], F32, name="gain")
+            recip = recips[pair + 1 - pair % 2]
+            engine.tensor_tensor(out=gain[:], in0=recip[:, pair % 2, :], in1=mask01[:, j, :], op=ALU.mult)
+            gains[pair] = gain
+
+        def gains_of(pair, engine):
+            before, j = pairs[pair - 1][1], pairs[pair][1]
+            gain = small.tile([P, 2, 2], F32, name="gains")
+            both = mask01[:, before : before + 2, :] if before < j else mask01[:, j : j + 1, :].to_broadcast([P, 2, 2])
+            engine.tensor_tensor(out=gain[:], in0=recips[pair][:], in1=both, op=ALU.mult)
+            gains[pair - 1], gains[pair] = gain[:, 0, :], gain[:, 1, :]
 
         SUMMED_TILES = ((1, 0), (1, 2), (1, 3))
         sums = {}
@@ -514,8 +524,10 @@ def tile_multiheadattentionlayer_pa_kernel(
                 quantise_values(item)
             if 2 <= s < 6:
                 compare_mask(s - 2, 1)
-            if s >= 2:
-                gain_of(s - 2)
+            if 2 <= s < 2 + TILES:
+                gain_of(s - 2, nc.gpsimd)
+            elif s >= 2 + TILES and s % 2 == 0:
+                gains_of(s - 1, nc.vector if s == n_pairs - 2 else nc.gpsimd)
             biased = [item for item in filled if item[0] == "v"]
             for item in biased:
                 add_bias(item)
@@ -565,8 +577,7 @@ def tile_multiheadattentionlayer_pa_kernel(
         rstd_by_scalar(nearly, None)
         reciprocal_of(last)
         quantise(last - 1)
-        for pair in (last - 1, last):
-            gain_of(pair)
+        gains_of(last, nc.vector)
         multiply(last - 1)
         for i in range(2):
             residual(last - 2, i)

import math
from contextlib import ExitStack

import concourse.mybir as mybir
from concourse.masks import make_identity

BF16 = mybir.dt.bfloat16
F32 = mybir.dt.float32
I32 = mybir.dt.int32
U32 = mybir.dt.uint32
U8 = mybir.dt.uint8
FP8X4 = mybir.dt.float8_e4m3fn_x4
ALU = mybir.AluOpType
ACT = mybir.ActivationFunctionType
AXIS_X = mybir.AxisListType.X

P = 128
PACK = 4
B, S, D, H = 2, 512, 1024, 8
DH = D // H
TILES = S // P
K_PASSES = D // (P * PACK)
SCORE_SCALE = 1.0 / math.sqrt(DH)
LN_EPS = 1e-8

FLOPS = 2 * B * S * D * D + 2 * (2 * B * H * S * S * DH)


def tile_multiheadattentionlayer_pa_kernel(
    tc, q_relu, k_relu, keys, Wv_words, Wv_scales, bv, queries, ln_gamma, ln_beta, out
):
    nc = tc.nc
    with ExitStack() as ctx:
        keep = ctx.enter_context(tc.tile_pool(name="keep", bufs=1))
        stage = ctx.enter_context(tc.tile_pool(name="stage", bufs=3))
        work = ctx.enter_context(tc.tile_pool(name="work", bufs=3))
        rows = ctx.enter_context(tc.tile_pool(name="rows", bufs=6))
        small = ctx.enter_context(tc.tile_pool(name="small", bufs=6))
        psum_s = ctx.enter_context(tc.psum_pool(name="psum_s", bufs=4))
        psum_t = ctx.enter_context(tc.psum_pool(name="psum_t", bufs=1))
        psum_o = ctx.enter_context(tc.psum_pool(name="psum_o", bufs=1))
        psum_p = ctx.enter_context(tc.psum_pool(name="psum_p", bufs=2))
        ctx.enter_context(tc.manual_schedule())

        HALF = D // 2
        k_sb = [keep.tile([P, TILES, D], BF16, name="k_sb" + str(b)) for b in range(B)]
        q_sb = [keep.tile([P, TILES, D], BF16, name="q_sb" + str(b)) for b in range(B)]
        x_sb = [keep.tile([P, TILES, D], BF16, name="x_sb" + str(b)) for b in range(B)]
        keys_sb = [keep.tile([P, TILES, D], BF16, name="keys_sb" + str(b)) for b in range(B)]
        w_scales = keep.tile([P, K_PASSES, D], U8, align_bytes=64)
        w_codes = keep.tile([P, K_PASSES, D], U32, align_bytes=64)
        bv_row = keep.tile([P, D], BF16)
        gamma_bc = keep.tile([P, D], BF16)
        beta_bc = keep.tile([P, D], BF16)

        def load_k(b, cols):
            nc.sync.dma_start(out=k_sb[b][:, :, cols], in_=k_relu[b].rearrange("(j p) d -> p j d", j=TILES)[:, :, cols])

        def load_q(b, cols, slots=slice(0, TILES)):
            nc.sync.dma_start(
                out=q_sb[b][:, slots, cols], in_=q_relu[b].rearrange("(p j) d -> p j d", j=TILES)[:, slots, cols]
            )

        def load_x(b, slots):
            nc.sync.dma_start(out=x_sb[b][:, slots, :], in_=queries[b].rearrange("(p j) d -> p j d", j=TILES)[:, slots, :])

        def load_keys(b):
            for u in range(2):
                nc.sync.dma_start(
                    out=keys_sb[b][:, 2 * u : 2 * u + 2, :],
                    in_=keys[b].rearrange("(u p e) d -> p u e d", u=2, e=2)[:, u, :, :],
                )

        warm = keep.tile([P, 1], F32)
        nc.vector.memset(warm[:], 1.0)
        warm_out = keep.tile([P, 1], F32)
        nc.scalar.activation(out=warm_out[:], in_=warm[:], func=ACT.Exp)
        ones = keep.tile([P, P], BF16)
        nc.vector.memset(ones[:], 1.0)
        zeros = keep.tile([P, HALF], BF16)
        nc.vector.memset(zeros[:], 0.0)
        nc.vector.memset(bv_row[:], 0.0)
        nc.vector.memset(w_scales[:].rearrange("p g n -> p (g n)").bitcast(I32), 0)

        load_k(0, slice(0, HALF // 2))
        for slots in (slice(0, 1), slice(1, TILES)):
            load_q(0, slice(0, HALF // 2), slots)
        nc.sync.dma_start(out=bv_row[0:1, :], in_=bv.rearrange("(o n) -> o n", o=1))
        load_x(0, slice(0, 1))
        for quad in range(4):
            nc.sync.dma_start(
                out=w_scales[32 * quad : 32 * quad + 4, :, :].bitcast(I32),
                in_=Wv_scales[:, 4 * quad : 4 * quad + 4, :].rearrange("g r n -> r g n").bitcast(I32),
            )
        load_keys(0)
        load_x(1, slice(0, 1))
        load_k(0, slice(HALF // 2, HALF))
        load_q(0, slice(HALF // 2, HALF))
        for g in range(K_PASSES):
            nc.sync.dma_start(
                out=w_codes[:, g, :].bitcast(I32),
                in_=Wv_words[g].rearrange("p n t -> p (n t)").bitcast(I32),
            )
        for b in range(B):
            load_x(b, slice(1, 2))
        load_k(0, slice(HALF, D))
        load_q(0, slice(HALF, D))
        for b in range(B):
            load_x(b, slice(2, 4))
        load_keys(1)
        load_k(1, slice(0, D))
        load_q(1, slice(0, D))
        nc.sync.dma_start(out=gamma_bc[:], in_=ln_gamma.partition_broadcast(P))
        nc.sync.dma_start(out=beta_bc[:], in_=ln_beta.partition_broadcast(P))

        ident_bf = keep.tile([P, P], BF16)
        make_identity(nc, ident_bf[:])
        ident_f32 = keep.tile([P, P], F32)
        make_identity(nc, ident_f32[:])
        neg_half = keep.tile([P, 1], F32)
        nc.gpsimd.memset(neg_half[:], -0.5)

        qT = keep.tile([P, B, H, TILES, P], BF16)
        kT = keep.tile([P, B, H, TILES, P], BF16)
        keys_grouped = [
            keep.tile([P, K_PASSES, S, PACK], BF16, align_bytes=64, name="keys_grouped" + str(b)) for b in range(B)
        ]
        keys_codes = keep.tile([P, K_PASSES, B, S], U32, align_bytes=64)
        keys_scales = keep.tile([P, K_PASSES, B, S], U8, align_bytes=64)
        v_codes = keep.tile([P, B, D], U32, align_bytes=64)
        v_scales = keep.tile([P, B, D], U8, align_bytes=64)
        abs_sum = keep.tile([P, TILES, B], F32)
        mask01 = keep.tile([P, TILES, B], F32)
        bv_bc = keep.tile([P, D], BF16)
        banks, groupeds = {}, {}

        def tensor_heads(item):
            kind, b, h0 = item
            source = k_sb[b] if kind == "k" else q_sb[b]
            pool, tag = (psum_o, "o_ps") if item == ("k", 0, 2) else (psum_p, "prep")
            banks[item] = pool.tile([P, 2, TILES, P], BF16, tag=tag, name="headsT")
            for i in range(2):
                for j in range(TILES):
                    nc.tensor.transpose(
                        banks[item][:, i, j, :], source[:, j, (h0 + i) * DH : (h0 + i + 1) * DH], ident_bf[:]
                    )

        def empty_heads(item):
            kind, b, h0 = item
            target = kT if kind == "k" else qT
            nc.scalar.copy(out=target[:, b, h0 : h0 + 2, :, :], in_=banks[item][:])

        def tensor_keys(item):
            kind, b, j = item
            keys_words = keys_sb[b][:, j, :].bitcast(F32)
            pool, tag = (psum_t, "eT") if item == ("x", 0, 2) else (psum_p, "prep")
            banks[item] = pool.tile([P, K_PASSES, 2, P], F32, tag=tag, name="keysT")
            for g in range(K_PASSES):
                for u in range(2):
                    nc.tensor.transpose(
                        banks[item][:, g, u, :], keys_words[:, 256 * g + u : 256 * (g + 1) : 2], ident_f32[:]
                    )

        def empty_keys(item):
            kind, b, j = item
            copy = nc.vector.tensor_copy if (b, j) in VECTOR_KEYS else nc.scalar.copy
            copy(
                out=keys_grouped[b][:].bitcast(F32)[:, :, j * P : (j + 1) * P, :],
                in_=banks[item][:].rearrange("p g u q -> p g q u"),
            )

        VECTOR_KEYS = ((0, 0), (0, 1), (0, 2), (0, 3))

        def quantise_keys(b, g):
            nc.vector.quantize_mx(
                out=keys_codes[:, g, b, :].bitcast(FP8X4),
                scales=keys_scales[:, g, b, :],
                in_=keys_grouped[b][:, g, :, :].rearrange("p q t -> p (q t)"),
            )

        def tensor_values(item):
            kind, b, h = item
            cols = slice(h * DH, (h + 1) * DH)
            banks[item] = psum_p.tile([P, TILES, DH], F32, tag="prep", name="v_ps")
            for j in range(TILES):
                toks = slice(j * P, (j + 1) * P)
                for g in range(K_PASSES):
                    nc.tensor.matmul_mx(
                        out=banks[item][:, j, :],
                        lhsT=keys_codes[:, g, b, toks].bitcast(FP8X4),
                        lhsT_scale=keys_scales[:, g, b, toks],
                        rhs=w_codes[:, g, cols].bitcast(FP8X4),
                        rhs_scale=w_scales[:, g, cols],
                        start=(g == 0),
                        stop=(g == K_PASSES - 1),
                    )

        def add_bias(item):
            kind, b, h = item
            groupeds[item] = stage.tile([P, DH, PACK], BF16, align_bytes=64, name="v_grouped")
            nc.vector.tensor_tensor(
                out=groupeds[item][:],
                in0=banks[item][:].rearrange("p j c -> p c j"),
                in1=bv_bc[:, h * DH : (h + 1) * DH].unsqueeze(2).to_broadcast([P, DH, PACK]),
                op=ALU.add,
            )

        def relu(item):
            v_flat = groupeds[item][:].rearrange("p c j -> p (c j)")
            nc.vector.tensor_scalar_max(v_flat, v_flat, 0.0)

        def quantise_values(item):
            kind, b, h = item
            cols = slice(h * DH, (h + 1) * DH)
            nc.vector.quantize_mx(
                out=v_codes[:, b, cols].bitcast(FP8X4),
                scales=v_scales[:, b, cols],
                in_=groupeds[item][:].rearrange("p c j -> p (c j)"),
            )

        tensor_part = {"k": tensor_heads, "q": tensor_heads, "x": tensor_keys, "v": tensor_values}

        def mask_on_vector(j, bb):
            nonzero = stage.tile([P, D], BF16, name="nonzero")
            nc.vector.tensor_scalar(
                out=nonzero[:],
                in0=x_sb[bb][:, j, :],
                scalar1=0.0,
                scalar2=None,
                op0=ALU.not_equal,
                op1=ALU.max,
                accum_out=mask01[:, j, bb : bb + 1],
            )

        def mask_on_scalar(j, bb):
            abs_x = stage.tile([P, D], BF16, name="abs_x")
            nc.scalar.activation(
                out=abs_x[:], in_=x_sb[bb][:, j, :], func=ACT.Abs, accum_out=abs_sum[:, j, bb : bb + 1]
            )

        def compare_mask(j, bb):
            nc.vector.tensor_single_scalar(mask01[:, j, bb : bb + 1], abs_sum[:, j, bb : bb + 1], 0.0, op=ALU.is_gt)

        pairs = []
        for b, js in ((0, (0, 1, 2, 3)), (1, (0, 1)), (1, (2,)), (1, (3,))):
            pairs += [(b, j, h0) for h0 in range(0, H, 2) for j in js]
        n_pairs = len(pairs)
        QUARTER = D // 4
        scores, rowmaxs, shifts, rowsums, es, eTs, e_groupeds, quantised, outputs = {}, {}, {}, {}, {}, {}, {}, {}, {}
        recips, gains, ys, stats, means, neg_means, rstds, normeds = {}, {}, {}, {}, {}, {}, {}, {}

        V_PAUSE = (7, 8)

        FREE_FROM = B * H + 3

        def score(pair, i):
            b, j, h0 = pairs[pair]
            scores[pair, i] = psum_s.tile([P, S], F32, tag="s_ps", name="s_ps")
            if i == 0 and (pair - 2 in V_PAUSE or pair - 2 >= B * H):
                nc.tensor.matmul_mx(
                    out=scores[pair, i][:, 0:512],
                    lhsT=w_codes[:, 0, 0:P].bitcast(FP8X4),
                    lhsT_scale=w_scales[:, 0, 0:P],
                    rhs=w_codes[:, 0, 0:512].bitcast(FP8X4),
                    rhs_scale=w_scales[:, 0, 0:512],
                    start=True,
                    stop=True,
                )
            nc.tensor.matmul(
                scores[pair, i][:],
                lhsT=qT[:, b, h0 + i, j, :],
                rhs=kT[:, b, h0 + i, :, :].rearrange("p t k -> p (t k)"),
                start=True,
                stop=True,
            )

        def row_max(pair, i):
            if i == 0:
                rowmaxs[pair] = small.tile([P, 2], F32, name="rowmax")
            nc.vector.tensor_reduce(out=rowmaxs[pair][:, i : i + 1], in_=scores[pair, i][:], axis=AXIS_X, op=ALU.max)

        def shift_of(pair):
            shifts[pair] = small.tile([P, 2], F32, name="shift")
            nc.scalar.mul(shifts[pair][:], rowmaxs[pair][:], -SCORE_SCALE)

        def exponentiate(pair, i):
            if i == 0:
                es[pair] = work.tile([P, 2, S], BF16, name="e")
                if pair % 2 == 0:
                    rowsums[pair] = small.tile([P, 4], F32, name="rowsum")
                else:
                    rowsums[pair] = rowsums[pair - 1]
            nc.scalar.activation(
                out=es[pair][:, i, :],
                in_=scores[pair, i][:],
                func=ACT.Exp,
                bias=shifts[pair][:, i : i + 1],
                scale=SCORE_SCALE,
                accum_out=rowsums[pair][:, 2 * (pair % 2) + i : 2 * (pair % 2) + i + 1],
            )

        def transpose_e(pair, i):
            if i == 0:
                pool, tag = (psum_p, "prep") if pair >= FREE_FROM and pair % 2 == 1 else (psum_t, "eT")
                eTs[pair] = pool.tile([P, 2, 2, P], F32, tag=tag, name="eT")
            e_words = es[pair][:, i, :].bitcast(F32)
            for u in range(2):
                nc.tensor.transpose(eTs[pair][:, i, u, :], e_words[:, u * P : (u + 1) * P], ident_f32[:])

        def regroup(pair):
            e_groupeds[pair] = work.tile([P, 2, P, PACK], BF16, align_bytes=64, name="e_grouped")
            nc.scalar.copy(out=e_groupeds[pair][:].bitcast(F32), in_=eTs[pair][:].rearrange("p i u q -> p i q u"))

        def quantise(pair):
            e_codes = work.tile([P, 2 * P], U32, align_bytes=64, name="e_codes")
            e_scales = work.tile([P, 2 * P], U8, align_bytes=64, name="e_scales")
            nc.vector.quantize_mx(
                out=e_codes[:].bitcast(FP8X4),
                scales=e_scales[:],
                in_=e_groupeds[pair][:].rearrange("p i q t -> p (i q t)"),
            )
            quantised[pair] = (e_codes, e_scales)

        def multiply(pair):
            b, j, h0 = pairs[pair]
            e_codes, e_scales = quantised[pair]
            pool, tag = (psum_p, "prep") if pair >= FREE_FROM and pair % 2 == 1 else (psum_o, "o_ps")
            outputs[pair] = pool.tile([P, 2, DH], F32, tag=tag, name="o_ps")
            for i in range(2):
                cols = slice((h0 + i) * DH, (h0 + i + 1) * DH)
                nc.tensor.matmul_mx(
                    out=outputs[pair][:, i, :],
                    lhsT=e_codes[:, i * P : (i + 1) * P].bitcast(FP8X4),
                    lhsT_scale=e_scales[:, i * P : (i + 1) * P],
                    rhs=v_codes[:, b, cols].bitcast(FP8X4),
                    rhs_scale=v_scales[:, b, cols],
                    start=True,
                    stop=True,
                )

        def reciprocal_of(pair):
            recips[pair] = small.tile([P, 2, 2], F32, name="recip")
            nc.vector.reciprocal(out=recips[pair][:].rearrange("p a i -> p (a i)"), in_=rowsums[pair][:])

        def gain_of(pair, engine):
            j = pairs[pair][1]
            gain = small.tile([P, 2], F32, name="gain")
            recip = recips[pair + 1 - pair % 2]
            engine.tensor_tensor(out=gain[:], in0=recip[:, pair % 2, :], in1=mask01[:, j, :], op=ALU.mult)
            gains[pair] = gain

        def gains_of(pair, engine):
            before, j = pairs[pair - 1][1], pairs[pair][1]
            gain = small.tile([P, 2, 2], F32, name="gains")
            both = mask01[:, before : before + 2, :] if before < j else mask01[:, j : j + 1, :].to_broadcast([P, 2, 2])
            engine.tensor_tensor(out=gain[:], in0=recips[pair][:], in1=both, op=ALU.mult)
            gains[pair - 1], gains[pair] = gain[:, 0, :], gain[:, 1, :]

        SUMMED_TILES = ((1, 0), (1, 2), (1, 3))
        sums = {}

        def residual(pair, i):
            b, j, h0 = pairs[pair]
            if h0 == 0 and i == 0:
                ys[b, j] = rows.tile([P, D], F32, name="y")
                if (b, j) in SUMMED_TILES:
                    sums[b, j] = small.tile([P, H], F32, name="sums")
            cols = slice((h0 + i) * DH, (h0 + i + 1) * DH)
            nc.vector.scalar_tensor_tensor(
                out=ys[b, j][:, cols],
                in0=outputs[pair][:, i, :],
                scalar=gains[pair][:, i : i + 1],
                in1=x_sb[b][:, j, cols],
                op0=ALU.mult,
                op1=ALU.add,
                accum_out=sums[b, j][:, h0 + i : h0 + i + 1] if (b, j) in SUMMED_TILES else None,
            )

        def neg_mean_of(t, part):
            neg_means[t] = small.tile([P, 1], F32, name="neg_mean")
            source = sums[t] if t in SUMMED_TILES else ys[t]
            unused = stage.tile([P, D], BF16, name="unused")
            nc.scalar.activation(
                out=unused[:, : source.shape[1]], in_=source[:], func=ACT.Identity, scale=-1.0 / D, accum_out=neg_means[t][:]
            )

        def rstd_by_scalar(t, part):
            squares = small.tile([P, 1], F32, name="squares")
            unused = stage.tile([P, D], BF16, name="unused")
            nc.scalar.activation(
                out=unused[:], in_=ys[t][:], func=ACT.Square, bias=neg_means[t][:], accum_out=squares[:]
            )
            rstds[t] = small.tile([P, 1], F32, name="rstd")
            if t in ((B - 1, TILES - 2), (B - 1, TILES - 1)):
                nc.scalar.activation(
                    out=rstds[t][:], in_=squares[:], func=ACT.Abs_reciprocal_sqrt, scale=1.0 / D, bias=LN_EPS
                )
                return
            var_eps = small.tile([P, 1], F32, name="var_eps")
            nc.gpsimd.tensor_scalar(var_eps[:], squares[:], 1.0 / D, LN_EPS, op0=ALU.mult, op1=ALU.add)
            nc.gpsimd.tensor_tensor(out=rstds[t][:], in0=var_eps[:], in1=neg_half[:], op=ALU.pow)

        PARTS = (slice(0, HALF), slice(HALF, D), slice(0, D))

        def store(t, half):
            b, j = t
            cols = PARTS[half]
            nc.sync.dma_start(
                out=out[b].rearrange("(p j) d -> p j d", j=TILES)[:, j, cols], in_=normeds[t][:, cols]
            )

        def centre(t, half):
            if half != 1:
                normeds[t] = work.tile([P, D], F32, name="normed")
            cols = PARTS[half]
            nc.vector.scalar_tensor_tensor(
                out=normeds[t][:, cols],
                in0=ys[t][:, cols],
                scalar=neg_means[t][:],
                in1=gamma_bc[:, cols],
                op0=ALU.add,
                op1=ALU.mult,
            )

        def scale_and_store(t, half):
            cols = PARTS[half]
            nc.vector.scalar_tensor_tensor(
                out=normeds[t][:, cols],
                in0=normeds[t][:, cols],
                scalar=rstds[t][:],
                in1=beta_bc[:, cols],
                op0=ALU.mult,
                op1=ALU.add,
            )
            store(t, half)

        spare = psum_o.tile([P, HALF], F32, name="o_ps")

        def keep_warm(times):
            for i in range(times):
                nc.tensor.matmul(spare[:], lhsT=ones[:], rhs=zeros[:], start=True, stop=True)

        keep_warm(5)

        def first_heads(source, target, pool, tag, heads, slots, copy):
            bank = pool.tile([P, len(heads), len(slots), P], BF16, tag=tag, name="first_heads")
            for i, h in enumerate(heads):
                for m, j in enumerate(slots):
                    nc.tensor.transpose(bank[:, i, m, :], source[:, j, h * DH : (h + 1) * DH], ident_bf[:])
            copy(out=target[:, 0, heads[0] : heads[-1] + 1, slots[0] : slots[-1] + 1, :], in_=bank[:])

        first_heads(k_sb[0], kT, psum_p, "prep", (0,), (0, 1, 2, 3), nc.scalar.copy)
        first_heads(k_sb[0], kT, psum_p, "prep", (1,), (0, 1, 2, 3), nc.vector.tensor_copy)
        first_heads(q_sb[0], qT, psum_t, "eT", (0, 1), (0,), nc.scalar.copy)
        first_heads(q_sb[0], qT, psum_s, "s_ps", (0, 1), (1, 2, 3), nc.vector.tensor_copy)
        for i in range(2):
            score(0, i)
        for c in range(2):
            pool, tag = ((psum_t, "eT"), (psum_p, "prep"))[c]
            bv_ps = pool.tile([P, HALF], F32, tag=tag, name="bv_ps")
            nc.tensor.matmul(
                bv_ps[:], lhsT=ones[:], rhs=bv_row[:, c * HALF : (c + 1) * HALF], start=True, stop=True
            )
            nc.scalar.copy(out=bv_bc[:, c * HALF : (c + 1) * HALF], in_=bv_ps[:])
        for i in range(2):
            score(1, i)
        for i in range(2):
            row_max(0, i)
        mask_on_vector(0, 0)
        for i in range(2):
            row_max(1, i)
        shift_of(0)
        for i in range(2):
            exponentiate(0, i)
        mask_on_scalar(0, 1)
        shift_of(1)
        exponentiate(1, 0)
        for j in range(TILES):
            tensor_keys(("x", 0, j))
            empty_keys(("x", 0, j))
            keep_warm(1)
        exponentiate(1, 1)
        first = [(kind, 0, 2) for kind in ("k", "q")]
        tensor_heads(first[0])
        for g in range(K_PASSES):
            quantise_keys(0, g)

        scalar_prep = [(kind, 0, 4) for kind in ("k", "q")]
        scalar_prep += [("x", 1, j) for j in range(TILES)]
        scalar_prep += [(kind, 0, 6) for kind in ("k", "q")]
        scalar_prep += [(kind, 1, h0) for h0 in range(0, H, 2) for kind in ("k", "q")]
        vector_prep = [("v", b, h) for b in range(B) for h in range(H)]

        vector_ln, scalar_ln = [], []
        filled, biased = first, []
        for s in range(n_pairs):
            if s >= 2:
                exponentiate(s, 0)
            if s >= 1:
                regroup(s - 1)
            if s >= 2:
                exponentiate(s, 1)
            if s + 2 < n_pairs:
                score(s + 2, 0)
            transpose_e(s, 0)
            transpose_e(s, 1)
            if s == 0:
                tensor_heads(first[1])
            if s + 2 < n_pairs:
                score(s + 2, 1)
            if s >= 2 and s % 2 == 0:
                reciprocal_of(s - 1)
            if 0 < s and s + 1 < n_pairs:
                row_max(s + 1, 0)
                row_max(s + 1, 1)
            if s >= 3:
                residual(s - 3, 0)
                residual(s - 3, 1)
            for item in biased:
                relu(item)
            if s >= 2:
                quantise(s - 2)
            for item in biased:
                quantise_values(item)
            if 2 <= s < 6:
                compare_mask(s - 2, 1)
            if 2 <= s < 2 + TILES:
                gain_of(s - 2, nc.gpsimd)
            elif s >= 2 + TILES and s % 2 == 0:
                gains_of(s - 1, nc.vector if s == n_pairs - 2 else nc.gpsimd)
            biased = [item for item in filled if item[0] == "v"]
            for item in biased:
                add_bias(item)
            if s == 8:
                for g in range(K_PASSES):
                    quantise_keys(1, g)
            pieces, vector_ln = vector_ln[:1], vector_ln[1:]
            for function, t, part in pieces:
                function(t, part)
            if 0 < s and s + 1 < n_pairs:
                shift_of(s + 1)
            pieces, scalar_ln = scalar_ln[:1], scalar_ln[1:]
            for function, t, part in pieces:
                function(t, part)
                apply = centre if function is neg_mean_of else scale_and_store
                vector_ln.append((apply, t, 2))
            for item in filled:
                if item[0] in ("k", "q"):
                    empty_heads(item)
                elif item[0] == "x":
                    empty_keys(item)
            if s >= 2:
                multiply(s - 2)
            take = 2 if s == 0 else 0 if s in V_PAUSE else 1
            filled, vector_prep = vector_prep[:take], vector_prep[take:]
            take = 1 if s > 0 else 0
            filled = filled + scalar_prep[:take]
            scalar_prep = scalar_prep[take:]
            for item in filled:
                tensor_part[item[0]](item)

            if 1 <= s < 5:
                if s > 1:
                    mask_on_vector(s - 1, 0)
                    mask_on_scalar(s - 1, 1)
            if s >= 3:
                b, j, h0 = pairs[s - 3]
                if h0 == H - 2 and (b, j) != (B - 1, TILES - 2):
                    scalar_ln += [(neg_mean_of, (b, j), None), (rstd_by_scalar, (b, j), None)]
        assert not (scalar_prep or vector_prep or filled or biased or scalar_ln or vector_ln)

        last = n_pairs - 1
        nearly, final = (B - 1, TILES - 2), (B - 1, TILES - 1)
        neg_mean_of(nearly, None)
        nc.scalar.activation(out=warm_out[:], in_=warm[:], func=ACT.Abs_reciprocal_sqrt)
        regroup(last)
        rstd_by_scalar(nearly, None)
        reciprocal_of(last)
        quantise(last - 1)
        gains_of(last, nc.vector)
        multiply(last - 1)
        for i in range(2):
            residual(last - 2, i)
        for i in range(2):
            residual(last - 1, i)
        centre(nearly, 0)
        quantise(last)
        multiply(last)
        centre(nearly, 1)
        for i in range(2):
            residual(last, i)
        neg_mean_of(final, None)
        rstd_by_scalar(final, None)
        scale_and_store(nearly, 0)
        for half in range(2):
            centre(final, half)
        scale_and_store(nearly, 1)
        for half in range(2):
            scale_and_store(final, half)
